import numpy as np
import ml_dtypes


def mxq(x, axis, fmt="e4m3"):
    dtype, down = {"e4m3": (ml_dtypes.float8_e4m3fn, 7), "e5m2": (ml_dtypes.float8_e5m2, 14)}[fmt]
    v = np.moveaxis(np.asarray(x, np.float32).astype(ml_dtypes.bfloat16).astype(np.float64), axis, -1)
    blocks = v.reshape(v.shape[:-1] + (-1, 32))
    amax = np.abs(blocks).max(-1, keepdims=True)
    byte = np.maximum(np.where(amax > 0, np.frexp(amax)[1] - 1 + 127, 0) - down, 1)
    scale = np.exp2(byte - 127.0)
    codes = (blocks / scale).astype(np.float32).astype(dtype).astype(np.float64)
    return np.moveaxis((codes * scale).reshape(v.shape), -1, axis)


WIDE = False


def mx_kscale(k):
    if not WIDE:
        return np.ones(k)
    levels = np.array([10, -10, 5, -5, 0])
    a = np.random.permutation(np.resize(levels, k // 512 * 4)).reshape(k // 512, 4)
    idx = np.arange(k)
    return np.exp2(a[idx // 512, idx % 128 // 32])


BF16 = ml_dtypes.bfloat16


def bf(x):
    return np.asarray(x, np.float32).astype(BF16)


def f64(x):
    return np.asarray(x).astype(np.float64)


B, H, O, I, K = 128, 1024, 128, 128, 512


def silu(v):
    return v / (1.0 + np.exp(-v))


def setup_inputs():
    s = mx_kscale(H)
    return {
        "hk": bf(silu(np.random.standard_normal((B, H))) * s),
        "kw2": bf(np.random.standard_normal((H, K)) * 1.5 / np.sqrt(H) / s[:, None]),
        "kb2": bf(np.random.standard_normal(K) * 0.3),
        "bases": bf(np.random.standard_normal((K, O, I)) * 1.5 / np.sqrt(K)),
        "base": bf(np.random.standard_normal((O, I)) * 0.7),
        "row": bf(1.0 + 0.1 * np.tanh(np.random.standard_normal((B, O)))),
        "col": bf(1.0 + 0.1 * np.tanh(np.random.standard_normal((B, I)))),
    }


def reference(hk, kw2, kb2, bases, base, row, col):
    coeff = np.tanh((mxq(f64(hk), 1, "e4m3") @ mxq(f64(kw2), 0, "e4m3")) + f64(kb2))
    delta = (mxq(coeff, 1, "e4m3") @ mxq(f64(bases).reshape(K, O * I), 0, "e4m3")).reshape(B, O, I)
    weight = (f64(base)[None] + delta) * f64(row)[:, :, None] * f64(col)[:, None, :]
    return weight, coeff

@@ -1,0 +1,281 @@
+from contextlib import ExitStack
+
+import concourse.mybir as mybir
+from concourse.masks import make_identity
+
+F32 = mybir.dt.float32
+BF16 = mybir.dt.bfloat16
+U32 = mybir.dt.uint32
+U8 = mybir.dt.uint8
+FP8X4 = mybir.dt.float8_e4m3fn_x4
+ADD = mybir.AluOpType.add
+MULT = mybir.AluOpType.mult
+TANH = mybir.ActivationFunctionType.Tanh
+
+P = 128
+PACK = 4
+K_PASS = P * PACK
+
+B, H, O, I, K = 128, 1024, 128, 128, 512
+N = O * I
+H_PASSES = H // K_PASS
+FLOPS = 2 * B * H * K + 2 * B * K * N
+
+UNIT = 512
+ROWS_PER_UNIT = UNIT // I
+LOAD_MAX = 2048
+RUN = 4
+VECTOR_COLUMNS = 128
+QUANTISE_AHEAD = 3
+REGROUP_AHEAD = 4
+RAW_BUFS = 3
+
+
+def cut_columns():
+    cuts = [(0, UNIT)]
+    while sum(cuts[-1]) < N:
+        start = sum(cuts[-1])
+        cuts.append((start, min(start, LOAD_MAX)))
+    return cuts
+
+
+def interleave(copy, grouped, rows):
+    copy(
+        out=grouped.rearrange("p (c i) j -> p c j i", i=RUN),
+        in_=rows.rearrange("p j (c i) -> p c j i", i=RUN),
+    )
+
+
+def tile_structuredternaryfactorgenerator_pa_kernel(
+    tc, hk, kw2, kb2, bases, base, row, col, out_0, out_1
+):
+    nc = tc.nc
+    cuts = cut_columns()
+    units = [
+        (l, offset) for l, (start, width) in enumerate(cuts) for offset in range(0, width, UNIT)
+    ]
+    n_units = len(units)
+
+    bases_rows = bases.rearrange("(p j) o i -> p j (o i)", j=PACK)
+    kw2_rows = kw2.rearrange("(c p j) n -> c p j n", c=H_PASSES, j=PACK)
+    base_flat = base.rearrange("o i -> (o i)")
+    weight_out = out_0.rearrange("b o i -> b (o i)")
+
+    with ExitStack() as ctx:
+        ctx.enter_context(tc.manual_schedule())
+        const = ctx.enter_context(tc.tile_pool(name="const", bufs=1))
+        raw_pool = ctx.enter_context(tc.tile_pool(name="raw", bufs=RAW_BUFS))
+        grouped_pool = ctx.enter_context(tc.tile_pool(name="grouped", bufs=3))
+        mx_pool = ctx.enter_context(tc.tile_pool(name="mx", bufs=3))
+        sum_pool = ctx.enter_context(tc.tile_pool(name="summed", bufs=3))
+        weight_pool = ctx.enter_context(tc.tile_pool(name="weight", bufs=3))
+        psum_acc = ctx.enter_context(tc.psum_pool(name="acc", bufs=6))
+        psum_tr = ctx.enter_context(tc.psum_pool(name="transposed", bufs=1))
+
+        raw, grouped, codes, scales, acc, summed, weight = {}, {}, {}, {}, {}, {}, {}
+        base_bc = const.tile([P, N], BF16)
+        coeff_codes = const.tile([P, B], U32, align_bytes=64)
+        coeff_scales = const.tile([P, B], U8, align_bytes=64)
+        row_f32 = const.tile([B, O], F32)
+        col_f32 = const.tile([B, I], F32)
+
+        def load(l):
+            start, width = cuts[l]
+            raw[l] = raw_pool.tile([P, PACK, width], BF16, name="raw", tag="raw")
+            nc.sync.dma_start(out=raw[l][:], in_=bases_rows[:, :, start : start + width])
+
+        def load_base(l):
+            start, width = cuts[l]
+            nc.sync.dma_start(
+                out=base_bc[:, start : start + width],
+                in_=base_flat[start : start + width].partition_broadcast(P),
+            )
+
+        def regroup(u):
+            l, offset = units[u]
+            width = cuts[l][1]
+            first = offset
+            if offset == 0:
+                grouped[l] = grouped_pool.tile(
+                    [P, width, PACK], BF16, name="grouped", tag="grouped", align_bytes=64
+                )
+                first = VECTOR_COLUMNS
+                interleave(nc.vector.tensor_copy, grouped[l][:, :first, :], raw[l][:, :, :first])
+            interleave(
+                nc.scalar.copy,
+                grouped[l][:, first : offset + UNIT, :],
+                raw[l][:, :, first : offset + UNIT],
+            )
+            if offset + UNIT == width:
+                if RAW_BUFS <= l + 1 < len(cuts):
+                    load_base(l + 1)
+                if l + RAW_BUFS < len(cuts):
+                    load(l + RAW_BUFS)
+
+        def quantise(u):
+            l, offset = units[u]
+            width = cuts[l][1]
+            if offset == 0:
+                codes[l] = mx_pool.tile([P, width], U32, name="codes", tag="codes", align_bytes=64)
+                scales[l] = mx_pool.tile([P, width], U8, name="scales", tag="scales", align_bytes=64)
+            nc.vector.quantize_mx(
+                out=codes[l][:, offset : offset + UNIT].bitcast(FP8X4),
+                scales=scales[l][:, offset : offset + UNIT],
+                in_=grouped[l][:, offset : offset + UNIT, :].rearrange("p w j -> p (w j)"),
+            )
+
+        def multiply(u):
+            l, offset = units[u]
+            acc[u] = psum_acc.tile([B, UNIT], F32, name="acc", tag="acc")
+            nc.tensor.matmul_mx(
+                out=acc[u][:],
+                lhsT=coeff_codes[:].bitcast(FP8X4),
+                lhsT_scale=coeff_scales[:],
+                rhs=codes[l][:, offset : offset + UNIT].bitcast(FP8X4),
+                rhs_scale=scales[l][:, offset : offset + UNIT],
+                start=True,
+                stop=True,
+            )
+
+        def add_base(u):
+            l, offset = units[u]
+            column = cuts[l][0] + offset
+            summed[u] = sum_pool.tile([B, UNIT], F32, name="summed", tag="summed")
+            nc.vector.tensor_tensor(
+                out=summed[u][:], in0=acc[u][:], in1=base_bc[:, column : column + UNIT], op=ADD
+            )
+
+        def apply_gains(u):
+            l, offset = units[u]
+            start, width = cuts[l]
+            if offset == 0:
+                weight[l] = weight_pool.tile([B, width], F32, name="weight", tag="weight")
+            for r in range(ROWS_PER_UNIT):
+                o = (start + offset) // I + r
+                nc.vector.scalar_tensor_tensor(
+                    out=weight[l][:, offset + r * I : offset + (r + 1) * I],
+                    in0=summed[u][:, r * I : (r + 1) * I],
+                    scalar=row_f32[:, o : o + 1],
+                    in1=col_f32[:],
+                    op0=MULT,
+                    op1=MULT,
+                )
+            if l == len(cuts) - 1:
+                column = start + offset
+                nc.sync.dma_start(
+                    out=weight_out[:, column : column + UNIT], in_=weight[l][:, offset : offset + UNIT]
+                )
+            elif offset + UNIT == width:
+                nc.gpsimd.dma_start(out=weight_out[:, start : start + width], in_=weight[l][:])
+
+        ident_f32 = const.tile([P, P], F32)
+        ident_bf16 = const.tile([P, P], BF16)
+        make_identity(nc, ident_f32[:])
+        make_identity(nc, ident_bf16[:])
+        warm = const.tile([P, 1], F32)
+        warmed = const.tile([P, 1], F32)
+        nc.vector.memset(warm[:], 0.0)
+        nc.scalar.activation(out=warmed[:], in_=warm[:], func=TANH)
+
+        hk_sb = const.tile([B, H], BF16)
+        kw2_raw = const.tile([P, H_PASSES, PACK, K], BF16)
+        kb2_bc = const.tile([B, K], BF16)
+        row_sb = const.tile([B, O], BF16)
+        col_sb = const.tile([B, I], BF16)
+        load(0)
+        nc.sync.dma_start(out=hk_sb[:], in_=hk)
+        nc.sync.dma_start(out=kw2_raw[:, 0], in_=kw2_rows[0])
+        load(1)
+        nc.sync.dma_start(out=kw2_raw[:, 1], in_=kw2_rows[1])
+        load(2)
+        nc.sync.dma_start(out=kb2_bc[:], in_=kb2.partition_broadcast(B))
+        nc.sync.dma_start(out=row_sb[:], in_=row)
+        nc.sync.dma_start(out=col_sb[:], in_=col)
+
+        regroup(0)
+        for l in range(RAW_BUFS):
+            load_base(l)
+
+        hk_words = hk_sb[:].bitcast(F32).rearrange("b (c p u) -> b c u p", c=H_PASSES, u=2)
+        hk_t = psum_tr.tile([P, H_PASSES, 2, B], F32)
+        for c in range(H_PASSES):
+            for u in range(2):
+                nc.tensor.transpose(hk_t[:, c, u, :], hk_words[:, c, u, :], ident_f32[:])
+        hk_grouped = const.tile([P, H_PASSES * B * PACK], BF16, align_bytes=64)
+        nc.vector.tensor_copy(
+            out=hk_grouped[:].bitcast(F32).rearrange("p (c b u) -> p c b u", c=H_PASSES, u=2),
+            in_=hk_t[:].rearrange("p c u b -> p c b u"),
+        )
+
+        kw2_grouped = const.tile([P, H_PASSES, K, PACK], BF16, align_bytes=64)
+        kw2_codes = const.tile([P, H_PASSES, K], U32, align_bytes=64)
+        kw2_scales = const.tile([P, H_PASSES, K], U8, align_bytes=64)
+        hk_codes = const.tile([P, H_PASSES * B], U32, align_bytes=64)
+        hk_scales = const.tile([P, H_PASSES * B], U8, align_bytes=64)
+
+        def quantise_kw2(c):
+            nc.vector.quantize_mx(
+                out=kw2_codes[:, c, :].bitcast(FP8X4),
+                scales=kw2_scales[:, c, :],
+                in_=kw2_grouped[:, c].rearrange("p n j -> p (n j)"),
+            )
+
+        interleave(nc.vector.tensor_copy, kw2_grouped[:, 0], kw2_raw[:, 0])
+        nc.vector.quantize_mx(out=hk_codes[:].bitcast(FP8X4), scales=hk_scales[:], in_=hk_grouped[:])
+        regroup(1)
+        interleave(nc.vector.tensor_copy, kw2_grouped[:, 1], kw2_raw[:, 1])
+        quantise_kw2(0)
+        quantise_kw2(1)
+
+        pre_acc = psum_acc.tile([B, K], F32, name="acc", tag="acc")
+        for c in range(H_PASSES):
+            nc.tensor.matmul_mx(
+                out=pre_acc[:],
+                lhsT=hk_codes[:, c * B : (c + 1) * B].bitcast(FP8X4),
+                lhsT_scale=hk_scales[:, c * B : (c + 1) * B],
+                rhs=kw2_codes[:, c, :].bitcast(FP8X4),
+                rhs_scale=kw2_scales[:, c, :],
+                start=(c == 0),
+                stop=(c == H_PASSES - 1),
+            )
+
+        regroup(2)
+        quantise(0)
+
+        pre = const.tile([B, K], F32)
+        coeff = const.tile([B, K], F32)
+        coeff_bf16 = const.tile([B, PACK, P], BF16)
+        nc.vector.tensor_tensor(out=pre[:], in0=pre_acc[:], in1=kb2_bc[:], op=ADD)
+        nc.scalar.activation(
+            out=coeff_bf16[:], in_=pre[:].rearrange("b (p t) -> b t p", t=PACK), func=TANH
+        )
+        nc.scalar.activation(out=coeff[:], in_=pre[:], func=TANH)
+        nc.gpsimd.dma_start(out=out_1, in_=coeff[:])
+        quantise(1)
+        nc.vector.tensor_copy(out=row_f32[:], in_=row_sb[:])
+        nc.vector.tensor_copy(out=col_f32[:], in_=col_sb[:])
+        coeff_t = psum_tr.tile([P, PACK, B], BF16)
+        for t in range(PACK):
+            nc.tensor.transpose(coeff_t[:, t, :], coeff_bf16[:, t, :], ident_bf16[:])
+        regroup(3)
+        coeff_grouped = const.tile([P, B, PACK], BF16, align_bytes=64)
+        nc.vector.tensor_copy(out=coeff_grouped[:], in_=coeff_t[:].rearrange("p t b -> p b t"))
+        quantise(2)
+        nc.vector.quantize_mx(
+            out=coeff_codes[:].bitcast(FP8X4),
+            scales=coeff_scales[:],
+            in_=coeff_grouped[:].rearrange("p b t -> p (b t)"),
+        )
+
+        for u in range(QUANTISE_AHEAD):
+            multiply(u)
+        add_base(0)
+        for u in range(n_units):
+            if u + REGROUP_AHEAD < n_units:
+                regroup(u + REGROUP_AHEAD)
+            if u + QUANTISE_AHEAD < n_units:
+                quantise(u + QUANTISE_AHEAD)
+                multiply(u + QUANTISE_AHEAD)
+            if u + 1 < n_units:
+                add_base(u + 1)
+            apply_gains(u)

@@ -25,10 +25,14 @@ UNIT = 512
 ROWS_PER_UNIT = UNIT // I
 LOAD_MAX = 2048
 RUN = 4
-VECTOR_COLUMNS = 128
+VECTOR_COLUMNS = 256
 QUANTISE_AHEAD = 3
 REGROUP_AHEAD = 4
 RAW_BUFS = 3
+BANK_ROWS = 8
+BASE_AHEAD = 4
+UNITS_PER_BANK = BANK_ROWS // ROWS_PER_UNIT
+N_BANKS = O // BANK_ROWS
 
 
 def cut_columns():
@@ -58,7 +62,6 @@ def tile_structuredternaryfactorgenerator_pa_kernel(
 
     bases_rows = bases.rearrange("(p j) o i -> p j (o i)", j=PACK)
     kw2_rows = kw2.rearrange("(c p j) n -> c p j n", c=H_PASSES, j=PACK)
-    base_flat = base.rearrange("o i -> (o i)")
     weight_out = out_0.rearrange("b o i -> b (o i)")
 
     with ExitStack() as ctx:
@@ -69,10 +72,14 @@ def tile_structuredternaryfactorgenerator_pa_kernel(
         mx_pool = ctx.enter_context(tc.tile_pool(name="mx", bufs=3))
         sum_pool = ctx.enter_context(tc.tile_pool(name="summed", bufs=3))
         weight_pool = ctx.enter_context(tc.tile_pool(name="weight", bufs=3))
-        psum_acc = ctx.enter_context(tc.psum_pool(name="acc", bufs=6))
+        psum_acc = ctx.enter_context(tc.psum_pool(name="acc", bufs=5))
         psum_tr = ctx.enter_context(tc.psum_pool(name="transposed", bufs=1))
+        psum_base = ctx.enter_context(tc.psum_pool(name="base_bank", bufs=2))
 
-        raw, grouped, codes, scales, acc, summed, weight = {}, {}, {}, {}, {}, {}, {}
+        raw, grouped, codes, scales, acc, summed, weight, base_bank = {}, {}, {}, {}, {}, {}, {}, {}
+        ident_f32 = const.tile([P, P], F32)
+        ident_bf16 = const.tile([P, P], BF16)
+        base_t = const.tile([I, O], BF16)
         base_bc = const.tile([P, N], BF16)
         coeff_codes = const.tile([P, B], U32, align_bytes=64)
         coeff_scales = const.tile([P, B], U8, align_bytes=64)
@@ -84,11 +91,18 @@ def tile_structuredternaryfactorgenerator_pa_kernel(
             raw[l] = raw_pool.tile([P, PACK, width], BF16, name="raw", tag="raw")
             nc.sync.dma_start(out=raw[l][:], in_=bases_rows[:, :, start : start + width])
 
-        def load_base(l):
-            start, width = cuts[l]
-            nc.sync.dma_start(
-                out=base_bc[:, start : start + width],
-                in_=base_flat[start : start + width].partition_broadcast(P),
+        def spread_base(g):
+            base_bank[g] = psum_base.tile([P, BANK_ROWS, I], BF16, name="base_bank", tag="base_bank")
+            for r in range(BANK_ROWS):
+                o = g * BANK_ROWS + r
+                nc.tensor.transpose(
+                    base_bank[g][:, r, :], base_t[:, o : o + 1].to_broadcast([I, P]), ident_bf16[:]
+                )
+
+        def keep_base(g):
+            nc.scalar.copy(
+                out=base_bc[:, g * BANK_ROWS * I : (g + 1) * BANK_ROWS * I],
+                in_=base_bank[g][:].rearrange("p r i -> p (r i)"),
             )
 
         def regroup(u):
@@ -106,11 +120,8 @@ def tile_structuredternaryfactorgenerator_pa_kernel(
                 grouped[l][:, first : offset + UNIT, :],
                 raw[l][:, :, first : offset + UNIT],
             )
-            if offset + UNIT == width:
-                if RAW_BUFS <= l + 1 < len(cuts):
-                    load_base(l + 1)
-                if l + RAW_BUFS < len(cuts):
-                    load(l + RAW_BUFS)
+            if offset + UNIT == width and l + RAW_BUFS < len(cuts):
+                load(l + RAW_BUFS)
 
         def quantise(u):
             l, offset = units[u]
@@ -168,10 +179,8 @@ def tile_structuredternaryfactorgenerator_pa_kernel(
             elif offset + UNIT == width:
                 nc.gpsimd.dma_start(out=weight_out[:, start : start + width], in_=weight[l][:])
 
-        ident_f32 = const.tile([P, P], F32)
-        ident_bf16 = const.tile([P, P], BF16)
-        make_identity(nc, ident_f32[:])
         make_identity(nc, ident_bf16[:])
+        make_identity(nc, ident_f32[:])
         warm = const.tile([P, 1], F32)
         warmed = const.tile([P, 1], F32)
         nc.vector.memset(warm[:], 0.0)
@@ -182,6 +191,8 @@ def tile_structuredternaryfactorgenerator_pa_kernel(
         kb2_bc = const.tile([B, K], BF16)
         row_sb = const.tile([B, O], BF16)
         col_sb = const.tile([B, I], BF16)
+        base_sb = const.tile([O, I], BF16)
+        nc.sync.dma_start(out=base_sb[:], in_=base)
         load(0)
         nc.sync.dma_start(out=hk_sb[:], in_=hk)
         nc.sync.dma_start(out=kw2_raw[:, 0], in_=kw2_rows[0])
@@ -192,15 +203,22 @@ def tile_structuredternaryfactorgenerator_pa_kernel(
         nc.sync.dma_start(out=row_sb[:], in_=row)
         nc.sync.dma_start(out=col_sb[:], in_=col)
 
+        base_t_ps = psum_tr.tile([I, O], BF16, name="base_t_ps", tag="transposed")
+        nc.tensor.transpose(base_t_ps[:], base_sb[:], ident_bf16[:])
+        nc.vector.tensor_copy(out=base_t[:], in_=base_t_ps[:])
+        spread_base(0)
+        spread_base(1)
         regroup(0)
-        for l in range(RAW_BUFS):
-            load_base(l)
+        keep_base(0)
+        keep_base(1)
 
         hk_words = hk_sb[:].bitcast(F32).rearrange("b (c p u) -> b c u p", c=H_PASSES, u=2)
-        hk_t = psum_tr.tile([P, H_PASSES, 2, B], F32)
+        hk_t = psum_tr.tile([P, H_PASSES, 2, B], F32, name="hk_t", tag="transposed")
         for c in range(H_PASSES):
             for u in range(2):
                 nc.tensor.transpose(hk_t[:, c, u, :], hk_words[:, c, u, :], ident_f32[:])
+        spread_base(2)
+        spread_base(3)
         hk_grouped = const.tile([P, H_PASSES * B * PACK], BF16, align_bytes=64)
         nc.vector.tensor_copy(
             out=hk_grouped[:].bitcast(F32).rearrange("p (c b u) -> p c b u", c=H_PASSES, u=2),
@@ -223,6 +241,10 @@ def tile_structuredternaryfactorgenerator_pa_kernel(
         interleave(nc.vector.tensor_copy, kw2_grouped[:, 0], kw2_raw[:, 0])
         nc.vector.quantize_mx(out=hk_codes[:].bitcast(FP8X4), scales=hk_scales[:], in_=hk_grouped[:])
         regroup(1)
+        keep_base(2)
+        keep_base(3)
+        spread_base(4)
+        spread_base(5)
         interleave(nc.vector.tensor_copy, kw2_grouped[:, 1], kw2_raw[:, 1])
         quantise_kw2(0)
         quantise_kw2(1)
@@ -254,7 +276,7 @@ def tile_structuredternaryfactorgenerator_pa_kernel(
         quantise(1)
         nc.vector.tensor_copy(out=row_f32[:], in_=row_sb[:])
         nc.vector.tensor_copy(out=col_f32[:], in_=col_sb[:])
-        coeff_t = psum_tr.tile([P, PACK, B], BF16)
+        coeff_t = psum_tr.tile([P, PACK, B], BF16, name="coeff_t", tag="transposed")
         for t in range(PACK):
             nc.tensor.transpose(coeff_t[:, t, :], coeff_bf16[:, t, :], ident_bf16[:])
         regroup(3)
@@ -273,6 +295,11 @@ def tile_structuredternaryfactorgenerator_pa_kernel(
         for u in range(n_units):
             if u + REGROUP_AHEAD < n_units:
                 regroup(u + REGROUP_AHEAD)
+            g = u // UNITS_PER_BANK + BASE_AHEAD
+            if u % UNITS_PER_BANK == 0 and g < N_BANKS:
+                keep_base(g)
+                if g + 2 < N_BANKS:
+                    spread_base(g + 2)
             if u + QUANTISE_AHEAD < n_units:
                 quantise(u + QUANTISE_AHEAD)
                 multiply(u + QUANTISE_AHEAD)

@@ -22,25 +22,21 @@ H_PASSES = H // K_PASS
 FLOPS = 2 * B * H * K + 2 * B * K * N
 
 UNIT = 512
+N_UNITS = N // UNIT
 ROWS_PER_UNIT = UNIT // I
-LOAD_MAX = 2048
+LOAD_UNITS = 2
+N_LOADS = N_UNITS // LOAD_UNITS
+RAW_BUFS = 8
+STORE_UNITS = 4
 RUN = 4
-VECTOR_COLUMNS = 256
+GPSIMD_COLUMNS = 128
+GROUPED_BUFS = 8
 QUANTISE_AHEAD = 3
 REGROUP_AHEAD = 4
-RAW_BUFS = 3
 BANK_ROWS = 8
-BASE_AHEAD = 4
-UNITS_PER_BANK = BANK_ROWS // ROWS_PER_UNIT
 N_BANKS = O // BANK_ROWS
-
-
-def cut_columns():
-    cuts = [(0, UNIT)]
-    while sum(cuts[-1]) < N:
-        start = sum(cuts[-1])
-        cuts.append((start, min(start, LOAD_MAX)))
-    return cuts
+UNITS_PER_BANK = BANK_ROWS // ROWS_PER_UNIT
+BASE_AHEAD = 4
 
 
 def interleave(copy, grouped, rows):
@@ -54,11 +50,6 @@ def tile_structuredternaryfactorgenerator_pa_kernel(
     tc, hk, kw2, kb2, bases, base, row, col, out_0, out_1
 ):
     nc = tc.nc
-    cuts = cut_columns()
-    units = [
-        (l, offset) for l, (start, width) in enumerate(cuts) for offset in range(0, width, UNIT)
-    ]
-    n_units = len(units)
 
     bases_rows = bases.rearrange("(p j) o i -> p j (o i)", j=PACK)
     kw2_rows = kw2.rearrange("(c p j) n -> c p j n", c=H_PASSES, j=PACK)
@@ -68,13 +59,14 @@ def tile_structuredternaryfactorgenerator_pa_kernel(
         ctx.enter_context(tc.manual_schedule())
         const = ctx.enter_context(tc.tile_pool(name="const", bufs=1))
         raw_pool = ctx.enter_context(tc.tile_pool(name="raw", bufs=RAW_BUFS))
-        grouped_pool = ctx.enter_context(tc.tile_pool(name="grouped", bufs=3))
-        mx_pool = ctx.enter_context(tc.tile_pool(name="mx", bufs=3))
+        grouped_pool = ctx.enter_context(tc.tile_pool(name="grouped", bufs=GROUPED_BUFS))
+        mx_pool = ctx.enter_context(tc.tile_pool(name="mx", bufs=4))
         sum_pool = ctx.enter_context(tc.tile_pool(name="summed", bufs=3))
-        weight_pool = ctx.enter_context(tc.tile_pool(name="weight", bufs=3))
-        psum_acc = ctx.enter_context(tc.psum_pool(name="acc", bufs=5))
+        weight_pool = ctx.enter_context(tc.tile_pool(name="weight", bufs=4))
+        psum_acc = ctx.enter_context(tc.psum_pool(name="acc", bufs=4))
         psum_tr = ctx.enter_context(tc.psum_pool(name="transposed", bufs=1))
         psum_base = ctx.enter_context(tc.psum_pool(name="base_bank", bufs=2))
+        psum_col = ctx.enter_context(tc.psum_pool(name="col", bufs=1))
 
         raw, grouped, codes, scales, acc, summed, weight, base_bank = {}, {}, {}, {}, {}, {}, {}, {}
         ident_f32 = const.tile([P, P], F32)
@@ -84,12 +76,16 @@ def tile_structuredternaryfactorgenerator_pa_kernel(
         coeff_codes = const.tile([P, B], U32, align_bytes=64)
         coeff_scales = const.tile([P, B], U8, align_bytes=64)
         row_f32 = const.tile([B, O], F32)
-        col_f32 = const.tile([B, I], F32)
+        col_ps = psum_col.tile([B, I], BF16)
 
-        def load(l):
-            start, width = cuts[l]
-            raw[l] = raw_pool.tile([P, PACK, width], BF16, name="raw", tag="raw")
-            nc.sync.dma_start(out=raw[l][:], in_=bases_rows[:, :, start : start + width])
+        def load(queue, l, pieces):
+            raw[l] = raw_pool.tile([P, PACK, LOAD_UNITS * UNIT], BF16, name="raw", tag="raw")
+            width = LOAD_UNITS * UNIT // pieces
+            for offset in range(0, LOAD_UNITS * UNIT, width):
+                start = l * LOAD_UNITS * UNIT + offset
+                queue.dma_start(
+                    out=raw[l][:, :, offset : offset + width], in_=bases_rows[:, :, start : start + width]
+                )
 
         def spread_base(g):
             base_bank[g] = psum_base.tile([P, BANK_ROWS, I], BF16, name="base_bank", tag="base_bank")
@@ -105,79 +101,82 @@ def tile_structuredternaryfactorgenerator_pa_kernel(
                 in_=base_bank[g][:].rearrange("p r i -> p (r i)"),
             )
 
-        def regroup(u):
-            l, offset = units[u]
-            width = cuts[l][1]
-            first = offset
-            if offset == 0:
-                grouped[l] = grouped_pool.tile(
-                    [P, width, PACK], BF16, name="grouped", tag="grouped", align_bytes=64
-                )
-                first = VECTOR_COLUMNS
-                interleave(nc.vector.tensor_copy, grouped[l][:, :first, :], raw[l][:, :, :first])
-            interleave(
-                nc.scalar.copy,
-                grouped[l][:, first : offset + UNIT, :],
-                raw[l][:, :, first : offset + UNIT],
+        def unit_rows(u):
+            offset = u % LOAD_UNITS * UNIT
+            return raw[u // LOAD_UNITS][:, :, offset : offset + UNIT]
+
+        def regroup(u, copy):
+            grouped[u] = grouped_pool.tile(
+                [P, UNIT, PACK], BF16, name="grouped", tag="grouped", align_bytes=64
             )
-            if offset + UNIT == width and l + RAW_BUFS < len(cuts):
-                load(l + RAW_BUFS)
+            interleave(copy, grouped[u][:], unit_rows(u))
+
+        def regroup_shared(u):
+            l, offset = u // LOAD_UNITS, u % LOAD_UNITS * UNIT
+            grouped[u] = grouped_pool.tile(
+                [P, UNIT, PACK], BF16, name="grouped", tag="grouped", align_bytes=64
+            )
+            nc.gpsimd.tensor_scalar(
+                out=grouped[u][:, :GPSIMD_COLUMNS, :],
+                in0=unit_rows(u)[:, :, :GPSIMD_COLUMNS].rearrange("p j w -> p w j"),
+                scalar1=1.0,
+                scalar2=0.0,
+                op0=MULT,
+                op1=ADD,
+            )
+            interleave(nc.scalar.copy, grouped[u][:, GPSIMD_COLUMNS:, :], unit_rows(u)[:, :, GPSIMD_COLUMNS:])
+            if offset == 0 and 0 < l <= N_LOADS - RAW_BUFS:
+                load(nc.scalar, l - 1 + RAW_BUFS, 1)
 
         def quantise(u):
-            l, offset = units[u]
-            width = cuts[l][1]
-            if offset == 0:
-                codes[l] = mx_pool.tile([P, width], U32, name="codes", tag="codes", align_bytes=64)
-                scales[l] = mx_pool.tile([P, width], U8, name="scales", tag="scales", align_bytes=64)
+            codes[u] = mx_pool.tile([P, UNIT], U32, name="codes", tag="codes", align_bytes=64)
+            scales[u] = mx_pool.tile([P, UNIT], U8, name="scales", tag="scales", align_bytes=64)
             nc.vector.quantize_mx(
-                out=codes[l][:, offset : offset + UNIT].bitcast(FP8X4),
-                scales=scales[l][:, offset : offset + UNIT],
-                in_=grouped[l][:, offset : offset + UNIT, :].rearrange("p w j -> p (w j)"),
+                out=codes[u][:].bitcast(FP8X4),
+                scales=scales[u][:],
+                in_=grouped[u][:].rearrange("p w j -> p (w j)"),
             )
 
         def multiply(u):
-            l, offset = units[u]
             acc[u] = psum_acc.tile([B, UNIT], F32, name="acc", tag="acc")
             nc.tensor.matmul_mx(
                 out=acc[u][:],
                 lhsT=coeff_codes[:].bitcast(FP8X4),
                 lhsT_scale=coeff_scales[:],
-                rhs=codes[l][:, offset : offset + UNIT].bitcast(FP8X4),
-                rhs_scale=scales[l][:, offset : offset + UNIT],
+                rhs=codes[u][:].bitcast(FP8X4),
+                rhs_scale=scales[u][:],
                 start=True,
                 stop=True,
             )
 
         def add_base(u):
-            l, offset = units[u]
-            column = cuts[l][0] + offset
             summed[u] = sum_pool.tile([B, UNIT], F32, name="summed", tag="summed")
             nc.vector.tensor_tensor(
-                out=summed[u][:], in0=acc[u][:], in1=base_bc[:, column : column + UNIT], op=ADD
+                out=summed[u][:], in0=acc[u][:], in1=base_bc[:, u * UNIT : (u + 1) * UNIT], op=ADD
             )
 
         def apply_gains(u):
-            l, offset = units[u]
-            start, width = cuts[l]
+            s, offset = u // STORE_UNITS, u % STORE_UNITS * UNIT
             if offset == 0:
-                weight[l] = weight_pool.tile([B, width], F32, name="weight", tag="weight")
+                weight[s] = weight_pool.tile([B, STORE_UNITS * UNIT], F32, name="weight", tag="weight")
             for r in range(ROWS_PER_UNIT):
-                o = (start + offset) // I + r
+                o = u * ROWS_PER_UNIT + r
                 nc.vector.scalar_tensor_tensor(
-                    out=weight[l][:, offset + r * I : offset + (r + 1) * I],
+                    out=weight[s][:, offset + r * I : offset + (r + 1) * I],
                     in0=summed[u][:, r * I : (r + 1) * I],
                     scalar=row_f32[:, o : o + 1],
-                    in1=col_f32[:],
+                    in1=col_ps[:],
                     op0=MULT,
                     op1=MULT,
                 )
-            if l == len(cuts) - 1:
-                column = start + offset
+            if u >= N_UNITS - STORE_UNITS:
                 nc.sync.dma_start(
-                    out=weight_out[:, column : column + UNIT], in_=weight[l][:, offset : offset + UNIT]
+                    out=weight_out[:, u * UNIT : (u + 1) * UNIT], in_=weight[s][:, offset : offset + UNIT]
                 )
-            elif offset + UNIT == width:
-                nc.gpsimd.dma_start(out=weight_out[:, start : start + width], in_=weight[l][:])
+            elif offset == (STORE_UNITS - 1) * UNIT:
+                nc.sync.dma_start(
+                    out=weight_out[:, (u + 1 - STORE_UNITS) * UNIT : (u + 1) * UNIT], in_=weight[s][:]
+                )
 
         make_identity(nc, ident_bf16[:])
         make_identity(nc, ident_f32[:])
@@ -186,68 +185,63 @@ def tile_structuredternaryfactorgenerator_pa_kernel(
         nc.vector.memset(warm[:], 0.0)
         nc.scalar.activation(out=warmed[:], in_=warm[:], func=TANH)
 
+        base_sb = const.tile([O, I], BF16)
         hk_sb = const.tile([B, H], BF16)
         kw2_raw = const.tile([P, H_PASSES, PACK, K], BF16)
         kb2_bc = const.tile([B, K], BF16)
         row_sb = const.tile([B, O], BF16)
         col_sb = const.tile([B, I], BF16)
-        base_sb = const.tile([O, I], BF16)
         nc.sync.dma_start(out=base_sb[:], in_=base)
-        load(0)
         nc.sync.dma_start(out=hk_sb[:], in_=hk)
-        nc.sync.dma_start(out=kw2_raw[:, 0], in_=kw2_rows[0])
-        load(1)
-        nc.sync.dma_start(out=kw2_raw[:, 1], in_=kw2_rows[1])
-        load(2)
+        for c in range(H_PASSES):
+            nc.sync.dma_start(out=kw2_raw[:, c], in_=kw2_rows[c])
         nc.sync.dma_start(out=kb2_bc[:], in_=kb2.partition_broadcast(B))
-        nc.sync.dma_start(out=row_sb[:], in_=row)
         nc.sync.dma_start(out=col_sb[:], in_=col)
+        nc.sync.dma_start(out=row_sb[:], in_=row)
+        load(nc.sync, 0, LOAD_UNITS)
+        for l in range(1, RAW_BUFS):
+            load(nc.sync, l, 1)
 
         base_t_ps = psum_tr.tile([I, O], BF16, name="base_t_ps", tag="transposed")
         nc.tensor.transpose(base_t_ps[:], base_sb[:], ident_bf16[:])
         nc.vector.tensor_copy(out=base_t[:], in_=base_t_ps[:])
-        spread_base(0)
-        spread_base(1)
-        regroup(0)
-        keep_base(0)
-        keep_base(1)
 
         hk_words = hk_sb[:].bitcast(F32).rearrange("b (c p u) -> b c u p", c=H_PASSES, u=2)
         hk_t = psum_tr.tile([P, H_PASSES, 2, B], F32, name="hk_t", tag="transposed")
         for c in range(H_PASSES):
             for u in range(2):
                 nc.tensor.transpose(hk_t[:, c, u, :], hk_words[:, c, u, :], ident_f32[:])
-        spread_base(2)
-        spread_base(3)
+        for g in range(BASE_AHEAD):
+            if g >= 2:
+                keep_base(g - 2)
+            spread_base(g)
+
         hk_grouped = const.tile([P, H_PASSES * B * PACK], BF16, align_bytes=64)
+        hk_codes = const.tile([P, H_PASSES * B], U32, align_bytes=64)
+        hk_scales = const.tile([P, H_PASSES * B], U8, align_bytes=64)
+        kw2_grouped = const.tile([P, H_PASSES, K, PACK], BF16, align_bytes=64)
+        kw2_codes = const.tile([P, H_PASSES, K], U32, align_bytes=64)
+        kw2_scales = const.tile([P, H_PASSES, K], U8, align_bytes=64)
+        for c in range(H_PASSES):
+            interleave(nc.vector.tensor_copy, kw2_grouped[:, c], kw2_raw[:, c])
         nc.vector.tensor_copy(
             out=hk_grouped[:].bitcast(F32).rearrange("p (c b u) -> p c b u", c=H_PASSES, u=2),
             in_=hk_t[:].rearrange("p c u b -> p c b u"),
         )
-
-        kw2_grouped = const.tile([P, H_PASSES, K, PACK], BF16, align_bytes=64)
-        kw2_codes = const.tile([P, H_PASSES, K], U32, align_bytes=64)
-        kw2_scales = const.tile([P, H_PASSES, K], U8, align_bytes=64)
-        hk_codes = const.tile([P, H_PASSES * B], U32, align_bytes=64)
-        hk_scales = const.tile([P, H_PASSES * B], U8, align_bytes=64)
-
-        def quantise_kw2(c):
+        for c in range(H_PASSES):
             nc.vector.quantize_mx(
                 out=kw2_codes[:, c, :].bitcast(FP8X4),
                 scales=kw2_scales[:, c, :],
                 in_=kw2_grouped[:, c].rearrange("p n j -> p (n j)"),
             )
-
-        interleave(nc.vector.tensor_copy, kw2_grouped[:, 0], kw2_raw[:, 0])
         nc.vector.quantize_mx(out=hk_codes[:].bitcast(FP8X4), scales=hk_scales[:], in_=hk_grouped[:])
-        regroup(1)
-        keep_base(2)
-        keep_base(3)
-        spread_base(4)
-        spread_base(5)
-        interleave(nc.vector.tensor_copy, kw2_grouped[:, 1], kw2_raw[:, 1])
-        quantise_kw2(0)
-        quantise_kw2(1)
+
+        col_t_ps = psum_tr.tile([I, B], BF16, name="col_t_ps", tag="transposed")
+        col_t = const.tile([I, B], BF16)
+        nc.tensor.transpose(col_t_ps[:], col_sb[:], ident_bf16[:])
+        nc.vector.tensor_copy(out=col_t[:], in_=col_t_ps[:])
+        nc.tensor.transpose(col_ps[:], col_t[:], ident_bf16[:])
+        nc.vector.tensor_copy(out=row_f32[:], in_=row_sb[:])
 
         pre_acc = psum_acc.tile([B, K], F32, name="acc", tag="acc")
         for c in range(H_PASSES):
@@ -260,9 +254,10 @@ def tile_structuredternaryfactorgenerator_pa_kernel(
                 start=(c == 0),
                 stop=(c == H_PASSES - 1),
             )
-
-        regroup(2)
-        quantise(0)
+        regroup(0, nc.scalar.copy)
+        keep_base(BASE_AHEAD - 2)
+        keep_base(BASE_AHEAD - 1)
+        regroup(1, nc.vector.tensor_copy)
 
         pre = const.tile([B, K], F32)
         coeff = const.tile([B, K], F32)
@@ -272,37 +267,39 @@ def tile_structuredternaryfactorgenerator_pa_kernel(
             out=coeff_bf16[:], in_=pre[:].rearrange("b (p t) -> b t p", t=PACK), func=TANH
         )
         nc.scalar.activation(out=coeff[:], in_=pre[:], func=TANH)
-        nc.gpsimd.dma_start(out=out_1, in_=coeff[:])
-        quantise(1)
-        nc.vector.tensor_copy(out=row_f32[:], in_=row_sb[:])
-        nc.vector.tensor_copy(out=col_f32[:], in_=col_sb[:])
+        nc.sync.dma_start(out=out_1, in_=coeff[:])
+        quantise(0)
         coeff_t = psum_tr.tile([P, PACK, B], BF16, name="coeff_t", tag="transposed")
         for t in range(PACK):
             nc.tensor.transpose(coeff_t[:, t, :], coeff_bf16[:, t, :], ident_bf16[:])
-        regroup(3)
         coeff_grouped = const.tile([P, B, PACK], BF16, align_bytes=64)
         nc.vector.tensor_copy(out=coeff_grouped[:], in_=coeff_t[:].rearrange("p t b -> p b t"))
-        quantise(2)
         nc.vector.quantize_mx(
             out=coeff_codes[:].bitcast(FP8X4),
             scales=coeff_scales[:],
             in_=coeff_grouped[:].rearrange("p b t -> p (b t)"),
         )
+        spread_base(BASE_AHEAD)
+        spread_base(BASE_AHEAD + 1)
+        regroup_shared(2)
+        regroup_shared(3)
+        quantise(1)
+        quantise(2)
 
         for u in range(QUANTISE_AHEAD):
             multiply(u)
         add_base(0)
-        for u in range(n_units):
-            if u + REGROUP_AHEAD < n_units:
-                regroup(u + REGROUP_AHEAD)
+        for u in range(N_UNITS):
+            if u + REGROUP_AHEAD < N_UNITS:
+                regroup_shared(u + REGROUP_AHEAD)
             g = u // UNITS_PER_BANK + BASE_AHEAD
             if u % UNITS_PER_BANK == 0 and g < N_BANKS:
                 keep_base(g)
                 if g + 2 < N_BANKS:
                     spread_base(g + 2)
-            if u + QUANTISE_AHEAD < n_units:
+            if u + QUANTISE_AHEAD < N_UNITS:
                 quantise(u + QUANTISE_AHEAD)
                 multiply(u + QUANTISE_AHEAD)
-            if u + 1 < n_units:
+            if u + 1 < N_UNITS:
                 add_base(u + 1)
             apply_gains(u)

@@ -29,9 +29,10 @@ N_LOADS = N_UNITS // LOAD_UNITS
 RAW_BUFS = 8
 STORE_UNITS = 4
 RUN = 4
-GPSIMD_COLUMNS = 128
+GPSIMD_COLUMNS = 160
 GROUPED_BUFS = 8
-QUANTISE_AHEAD = 3
+QUANTISE_AHEAD = 2
+FIRST_UNITS = 3
 REGROUP_AHEAD = 4
 BANK_ROWS = 8
 N_BANKS = O // BANK_ROWS
@@ -211,12 +212,20 @@ def tile_structuredternaryfactorgenerator_pa_kernel(
         for c in range(H_PASSES):
             for u in range(2):
                 nc.tensor.transpose(hk_t[:, c, u, :], hk_words[:, c, u, :], ident_f32[:])
-        for g in range(BASE_AHEAD):
-            if g >= 2:
-                keep_base(g - 2)
+        hk_grouped = const.tile([P, H_PASSES * B * PACK], BF16, align_bytes=64)
+        nc.scalar.copy(
+            out=hk_grouped[:].bitcast(F32).rearrange("p (c b u) -> p c b u", c=H_PASSES, u=2),
+            in_=hk_t[:].rearrange("p c u b -> p c b u"),
+        )
+        spread_base(0)
+        spread_base(1)
+        col_t_ps = psum_tr.tile([I, B], BF16, name="col_t_ps", tag="transposed")
+        col_t = const.tile([I, B], BF16)
+        nc.tensor.transpose(col_t_ps[:], col_sb[:], ident_bf16[:])
+        for g in range(2, BASE_AHEAD):
+            keep_base(g - 2)
             spread_base(g)
 
-        hk_grouped = const.tile([P, H_PASSES * B * PACK], BF16, align_bytes=64)
         hk_codes = const.tile([P, H_PASSES * B], U32, align_bytes=64)
         hk_scales = const.tile([P, H_PASSES * B], U8, align_bytes=64)
         kw2_grouped = const.tile([P, H_PASSES, K, PACK], BF16, align_bytes=64)
@@ -224,10 +233,6 @@ def tile_structuredternaryfactorgenerator_pa_kernel(
         kw2_scales = const.tile([P, H_PASSES, K], U8, align_bytes=64)
         for c in range(H_PASSES):
             interleave(nc.vector.tensor_copy, kw2_grouped[:, c], kw2_raw[:, c])
-        nc.vector.tensor_copy(
-            out=hk_grouped[:].bitcast(F32).rearrange("p (c b u) -> p c b u", c=H_PASSES, u=2),
-            in_=hk_t[:].rearrange("p c u b -> p c b u"),
-        )
         for c in range(H_PASSES):
             nc.vector.quantize_mx(
                 out=kw2_codes[:, c, :].bitcast(FP8X4),
@@ -236,9 +241,6 @@ def tile_structuredternaryfactorgenerator_pa_kernel(
             )
         nc.vector.quantize_mx(out=hk_codes[:].bitcast(FP8X4), scales=hk_scales[:], in_=hk_grouped[:])
 
-        col_t_ps = psum_tr.tile([I, B], BF16, name="col_t_ps", tag="transposed")
-        col_t = const.tile([I, B], BF16)
-        nc.tensor.transpose(col_t_ps[:], col_sb[:], ident_bf16[:])
         nc.vector.tensor_copy(out=col_t[:], in_=col_t_ps[:])
         nc.tensor.transpose(col_ps[:], col_t[:], ident_bf16[:])
         nc.vector.tensor_copy(out=row_f32[:], in_=row_sb[:])
@@ -266,9 +268,8 @@ def tile_structuredternaryfactorgenerator_pa_kernel(
         nc.scalar.activation(
             out=coeff_bf16[:], in_=pre[:].rearrange("b (p t) -> b t p", t=PACK), func=TANH
         )
-        nc.scalar.activation(out=coeff[:], in_=pre[:], func=TANH)
-        nc.sync.dma_start(out=out_1, in_=coeff[:])
         quantise(0)
+        quantise(1)
         coeff_t = psum_tr.tile([P, PACK, B], BF16, name="coeff_t", tag="transposed")
         for t in range(PACK):
             nc.tensor.transpose(coeff_t[:, t, :], coeff_bf16[:, t, :], ident_bf16[:])
@@ -279,15 +280,17 @@ def tile_structuredternaryfactorgenerator_pa_kernel(
             scales=coeff_scales[:],
             in_=coeff_grouped[:].rearrange("p b t -> p (b t)"),
         )
-        spread_base(BASE_AHEAD)
-        spread_base(BASE_AHEAD + 1)
         regroup_shared(2)
         regroup_shared(3)
-        quantise(1)
-        quantise(2)
+        nc.scalar.activation(out=coeff[:], in_=pre[:], func=TANH)
+        nc.sync.dma_start(out=out_1, in_=coeff[:])
 
-        for u in range(QUANTISE_AHEAD):
-            multiply(u)
+        multiply(0)
+        multiply(1)
+        spread_base(BASE_AHEAD)
+        spread_base(BASE_AHEAD + 1)
+        quantise(2)
+        multiply(2)
         add_base(0)
         for u in range(N_UNITS):
             if u + REGROUP_AHEAD < N_UNITS:
@@ -295,11 +298,11 @@ def tile_structuredternaryfactorgenerator_pa_kernel(
             g = u // UNITS_PER_BANK + BASE_AHEAD
             if u % UNITS_PER_BANK == 0 and g < N_BANKS:
                 keep_base(g)
-                if g + 2 < N_BANKS:
-                    spread_base(g + 2)
-            if u + QUANTISE_AHEAD < N_UNITS:
+            if FIRST_UNITS <= u + QUANTISE_AHEAD < N_UNITS:
                 quantise(u + QUANTISE_AHEAD)
                 multiply(u + QUANTISE_AHEAD)
+            if u % UNITS_PER_BANK == 1 and g + 2 < N_BANKS:
+                spread_base(g + 2)
             if u + 1 < N_UNITS:
                 add_base(u + 1)
             apply_gains(u)

@@ -29,7 +29,7 @@ N_LOADS = N_UNITS // LOAD_UNITS
 RAW_BUFS = 8
 STORE_UNITS = 4
 RUN = 4
-GPSIMD_COLUMNS = 160
+GPSIMD_COLUMNS = 128
 GROUPED_BUFS = 8
 QUANTISE_AHEAD = 2
 FIRST_UNITS = 3
@@ -127,7 +127,7 @@ def tile_structuredternaryfactorgenerator_pa_kernel(
             )
             interleave(nc.scalar.copy, grouped[u][:, GPSIMD_COLUMNS:, :], unit_rows(u)[:, :, GPSIMD_COLUMNS:])
             if offset == 0 and 0 < l <= N_LOADS - RAW_BUFS:
-                load(nc.scalar, l - 1 + RAW_BUFS, 1)
+                load(nc.sync, l - 1 + RAW_BUFS, 1)
 
         def quantise(u):
             codes[u] = mx_pool.tile([P, UNIT], U32, name="codes", tag="codes", align_bytes=64)
@@ -282,8 +282,6 @@ def tile_structuredternaryfactorgenerator_pa_kernel(
         )
         regroup_shared(2)
         regroup_shared(3)
-        nc.scalar.activation(out=coeff[:], in_=pre[:], func=TANH)
-        nc.sync.dma_start(out=out_1, in_=coeff[:])
 
         multiply(0)
         multiply(1)
@@ -295,6 +293,9 @@ def tile_structuredternaryfactorgenerator_pa_kernel(
         for u in range(N_UNITS):
             if u + REGROUP_AHEAD < N_UNITS:
                 regroup_shared(u + REGROUP_AHEAD)
+            if u + REGROUP_AHEAD == N_UNITS:
+                nc.scalar.activation(out=coeff[:], in_=pre[:], func=TANH)
+                nc.sync.dma_start(out=out_1, in_=coeff[:])
             g = u // UNITS_PER_BANK + BASE_AHEAD
             if u % UNITS_PER_BANK == 0 and g < N_BANKS:
                 keep_base(g)

@@ -11,6 +11,7 @@ FP8X4 = mybir.dt.float8_e4m3fn_x4
 ADD = mybir.AluOpType.add
 MULT = mybir.AluOpType.mult
 TANH = mybir.ActivationFunctionType.Tanh
+COPY = mybir.ActivationFunctionType.Copy
 
 P = 128
 PACK = 4
@@ -23,21 +24,17 @@ FLOPS = 2 * B * H * K + 2 * B * K * N
 
 UNIT = 512
 N_UNITS = N // UNIT
-ROWS_PER_UNIT = UNIT // I
+ROWS = UNIT // I
 LOAD_UNITS = 2
 N_LOADS = N_UNITS // LOAD_UNITS
-RAW_BUFS = 8
-STORE_UNITS = 4
+RAW_BUFS = 10
+STORE_UNITS = 2
 RUN = 4
 GPSIMD_COLUMNS = 128
-GROUPED_BUFS = 8
+VECTOR_COLUMNS = 128
+AHEAD = 4
 QUANTISE_AHEAD = 2
-FIRST_UNITS = 3
-REGROUP_AHEAD = 4
-BANK_ROWS = 8
-N_BANKS = O // BANK_ROWS
-UNITS_PER_BANK = BANK_ROWS // ROWS_PER_UNIT
-BASE_AHEAD = 4
+FIRST = 2
 
 
 def interleave(copy, grouped, rows):
@@ -60,63 +57,41 @@ def tile_structuredternaryfactorgenerator_pa_kernel(
         ctx.enter_context(tc.manual_schedule())
         const = ctx.enter_context(tc.tile_pool(name="const", bufs=1))
         raw_pool = ctx.enter_context(tc.tile_pool(name="raw", bufs=RAW_BUFS))
-        grouped_pool = ctx.enter_context(tc.tile_pool(name="grouped", bufs=GROUPED_BUFS))
-        mx_pool = ctx.enter_context(tc.tile_pool(name="mx", bufs=4))
-        sum_pool = ctx.enter_context(tc.tile_pool(name="summed", bufs=3))
+        grouped_pool = ctx.enter_context(tc.tile_pool(name="grouped", bufs=8))
+        mx_pool = ctx.enter_context(tc.tile_pool(name="mx", bufs=5))
+        mid_pool = ctx.enter_context(tc.tile_pool(name="mid", bufs=3))
         weight_pool = ctx.enter_context(tc.tile_pool(name="weight", bufs=4))
-        psum_acc = ctx.enter_context(tc.psum_pool(name="acc", bufs=4))
-        psum_tr = ctx.enter_context(tc.psum_pool(name="transposed", bufs=1))
-        psum_base = ctx.enter_context(tc.psum_pool(name="base_bank", bufs=2))
-        psum_col = ctx.enter_context(tc.psum_pool(name="col", bufs=1))
+        psum_acc = ctx.enter_context(tc.psum_pool(name="acc", bufs=3))
+        psum_turned = ctx.enter_context(tc.psum_pool(name="turned", bufs=3))
+        psum_head = ctx.enter_context(tc.psum_pool(name="head", bufs=2))
 
-        raw, grouped, codes, scales, acc, summed, weight, base_bank = {}, {}, {}, {}, {}, {}, {}, {}
+        raw, grouped, codes, scales, acc, mid, turned, weight = {}, {}, {}, {}, {}, {}, {}, {}
         ident_f32 = const.tile([P, P], F32)
         ident_bf16 = const.tile([P, P], BF16)
-        base_t = const.tile([I, O], BF16)
-        base_bc = const.tile([P, N], BF16)
         coeff_codes = const.tile([P, B], U32, align_bytes=64)
         coeff_scales = const.tile([P, B], U8, align_bytes=64)
         row_f32 = const.tile([B, O], F32)
-        col_ps = psum_col.tile([B, I], BF16)
+        base_col_t = const.tile([P, 2, P], F32)
 
-        def load(queue, l, pieces):
+        def load(l, pieces):
             raw[l] = raw_pool.tile([P, PACK, LOAD_UNITS * UNIT], BF16, name="raw", tag="raw")
             width = LOAD_UNITS * UNIT // pieces
             for offset in range(0, LOAD_UNITS * UNIT, width):
                 start = l * LOAD_UNITS * UNIT + offset
-                queue.dma_start(
+                nc.sync.dma_start(
                     out=raw[l][:, :, offset : offset + width], in_=bases_rows[:, :, start : start + width]
                 )
-
-        def spread_base(g):
-            base_bank[g] = psum_base.tile([P, BANK_ROWS, I], BF16, name="base_bank", tag="base_bank")
-            for r in range(BANK_ROWS):
-                o = g * BANK_ROWS + r
-                nc.tensor.transpose(
-                    base_bank[g][:, r, :], base_t[:, o : o + 1].to_broadcast([I, P]), ident_bf16[:]
-                )
-
-        def keep_base(g):
-            nc.scalar.copy(
-                out=base_bc[:, g * BANK_ROWS * I : (g + 1) * BANK_ROWS * I],
-                in_=base_bank[g][:].rearrange("p r i -> p (r i)"),
-            )
 
         def unit_rows(u):
             offset = u % LOAD_UNITS * UNIT
             return raw[u // LOAD_UNITS][:, :, offset : offset + UNIT]
 
-        def regroup(u, copy):
+        def begin(u):
             grouped[u] = grouped_pool.tile(
                 [P, UNIT, PACK], BF16, name="grouped", tag="grouped", align_bytes=64
             )
-            interleave(copy, grouped[u][:], unit_rows(u))
 
-        def regroup_shared(u):
-            l, offset = u // LOAD_UNITS, u % LOAD_UNITS * UNIT
-            grouped[u] = grouped_pool.tile(
-                [P, UNIT, PACK], BF16, name="grouped", tag="grouped", align_bytes=64
-            )
+        def on_gpsimd(u):
             nc.gpsimd.tensor_scalar(
                 out=grouped[u][:, :GPSIMD_COLUMNS, :],
                 in0=unit_rows(u)[:, :, :GPSIMD_COLUMNS].rearrange("p j w -> p w j"),
@@ -125,9 +100,21 @@ def tile_structuredternaryfactorgenerator_pa_kernel(
                 op0=MULT,
                 op1=ADD,
             )
-            interleave(nc.scalar.copy, grouped[u][:, GPSIMD_COLUMNS:, :], unit_rows(u)[:, :, GPSIMD_COLUMNS:])
-            if offset == 0 and 0 < l <= N_LOADS - RAW_BUFS:
-                load(nc.sync, l - 1 + RAW_BUFS, 1)
+
+        def on_engine(copy, u, start, stop):
+            interleave(copy, grouped[u][:, start:stop, :], unit_rows(u)[:, :, start:stop])
+
+        def on_vector(u):
+            if u < FIRST:
+                on_engine(nc.vector.tensor_copy, u, 0, UNIT // 2)
+            else:
+                on_engine(nc.vector.tensor_copy, u, GPSIMD_COLUMNS, GPSIMD_COLUMNS + VECTOR_COLUMNS)
+
+        def on_scalar(u):
+            if u < FIRST:
+                on_engine(nc.scalar.copy, u, UNIT // 2, UNIT)
+            else:
+                on_engine(nc.scalar.copy, u, GPSIMD_COLUMNS + VECTOR_COLUMNS, UNIT)
 
         def quantise(u):
             codes[u] = mx_pool.tile([P, UNIT], U32, name="codes", tag="codes", align_bytes=64)
@@ -139,36 +126,48 @@ def tile_structuredternaryfactorgenerator_pa_kernel(
             )
 
         def multiply(u):
-            acc[u] = psum_acc.tile([B, UNIT], F32, name="acc", tag="acc")
-            nc.tensor.matmul_mx(
-                out=acc[u][:],
-                lhsT=coeff_codes[:].bitcast(FP8X4),
-                lhsT_scale=coeff_scales[:],
-                rhs=codes[u][:].bitcast(FP8X4),
-                rhs_scale=scales[u][:],
-                start=True,
-                stop=True,
-            )
+            acc[u] = psum_acc.tile([I, ROWS, B], F32, name="acc", tag="acc")
+            for r in range(ROWS):
+                cols = slice(r * I, (r + 1) * I)
+                nc.tensor.matmul_mx(
+                    out=acc[u][:, r, :],
+                    lhsT=codes[u][:, cols].bitcast(FP8X4),
+                    lhsT_scale=scales[u][:, cols],
+                    rhs=coeff_codes[:].bitcast(FP8X4),
+                    rhs_scale=coeff_scales[:],
+                    start=True,
+                    stop=True,
+                )
 
         def add_base(u):
-            summed[u] = sum_pool.tile([B, UNIT], F32, name="summed", tag="summed")
-            nc.vector.tensor_tensor(
-                out=summed[u][:], in0=acc[u][:], in1=base_bc[:, u * UNIT : (u + 1) * UNIT], op=ADD
-            )
+            mid[u] = mid_pool.tile([I, ROWS, B], F32, name="mid", tag="mid")
+            for r in range(ROWS):
+                o = u * ROWS + r
+                nc.vector.scalar_tensor_tensor(
+                    out=mid[u][:, r, :],
+                    in0=acc[u][:, r, :],
+                    scalar=base_col_t[:, 0, o : o + 1],
+                    in1=base_col_t[:, 1, :],
+                    op0=ADD,
+                    op1=MULT,
+                )
 
-        def apply_gains(u):
+        def turn(u):
+            turned[u] = psum_turned.tile([B, ROWS, I], F32, name="turned", tag="turned")
+            for r in range(ROWS):
+                nc.tensor.transpose(turned[u][:, r, :], mid[u][:, r, :], ident_f32[:])
+
+        def apply_row(u):
             s, offset = u // STORE_UNITS, u % STORE_UNITS * UNIT
             if offset == 0:
                 weight[s] = weight_pool.tile([B, STORE_UNITS * UNIT], F32, name="weight", tag="weight")
-            for r in range(ROWS_PER_UNIT):
-                o = u * ROWS_PER_UNIT + r
-                nc.vector.scalar_tensor_tensor(
+            for r in range(ROWS):
+                o = u * ROWS + r
+                nc.scalar.activation(
                     out=weight[s][:, offset + r * I : offset + (r + 1) * I],
-                    in0=summed[u][:, r * I : (r + 1) * I],
-                    scalar=row_f32[:, o : o + 1],
-                    in1=col_ps[:],
-                    op0=MULT,
-                    op1=MULT,
+                    in_=turned[u][:, r, :],
+                    func=COPY,
+                    scale=row_f32[:, o : o + 1],
                 )
             if u >= N_UNITS - STORE_UNITS:
                 nc.sync.dma_start(
@@ -179,36 +178,32 @@ def tile_structuredternaryfactorgenerator_pa_kernel(
                     out=weight_out[:, (u + 1 - STORE_UNITS) * UNIT : (u + 1) * UNIT], in_=weight[s][:]
                 )
 
-        make_identity(nc, ident_bf16[:])
-        make_identity(nc, ident_f32[:])
         warm = const.tile([P, 1], F32)
         warmed = const.tile([P, 1], F32)
         nc.vector.memset(warm[:], 0.0)
         nc.scalar.activation(out=warmed[:], in_=warm[:], func=TANH)
+        make_identity(nc, ident_f32[:])
+        make_identity(nc, ident_bf16[:])
 
-        base_sb = const.tile([O, I], BF16)
         hk_sb = const.tile([B, H], BF16)
         kw2_raw = const.tile([P, H_PASSES, PACK, K], BF16)
-        kb2_bc = const.tile([B, K], BF16)
-        row_sb = const.tile([B, O], BF16)
+        kb2_t = const.tile([P, PACK], BF16)
+        base_sb = const.tile([O, I], BF16)
         col_sb = const.tile([B, I], BF16)
-        nc.sync.dma_start(out=base_sb[:], in_=base)
+        row_sb = const.tile([B, O], BF16)
         nc.sync.dma_start(out=hk_sb[:], in_=hk)
         for c in range(H_PASSES):
             nc.sync.dma_start(out=kw2_raw[:, c], in_=kw2_rows[c])
-        nc.sync.dma_start(out=kb2_bc[:], in_=kb2.partition_broadcast(B))
+        nc.sync.dma_start(out=kb2_t[:], in_=kb2.rearrange("(p t) -> p t", t=PACK))
+        load(0, LOAD_UNITS)
+        nc.sync.dma_start(out=base_sb[:], in_=base)
         nc.sync.dma_start(out=col_sb[:], in_=col)
         nc.sync.dma_start(out=row_sb[:], in_=row)
-        load(nc.sync, 0, LOAD_UNITS)
         for l in range(1, RAW_BUFS):
-            load(nc.sync, l, 1)
-
-        base_t_ps = psum_tr.tile([I, O], BF16, name="base_t_ps", tag="transposed")
-        nc.tensor.transpose(base_t_ps[:], base_sb[:], ident_bf16[:])
-        nc.vector.tensor_copy(out=base_t[:], in_=base_t_ps[:])
+            load(l, 1)
 
         hk_words = hk_sb[:].bitcast(F32).rearrange("b (c p u) -> b c u p", c=H_PASSES, u=2)
-        hk_t = psum_tr.tile([P, H_PASSES, 2, B], F32, name="hk_t", tag="transposed")
+        hk_t = psum_head.tile([P, H_PASSES, 2, B], F32, name="hk_t", tag="head")
         for c in range(H_PASSES):
             for u in range(2):
                 nc.tensor.transpose(hk_t[:, c, u, :], hk_words[:, c, u, :], ident_f32[:])
@@ -217,93 +212,107 @@ def tile_structuredternaryfactorgenerator_pa_kernel(
             out=hk_grouped[:].bitcast(F32).rearrange("p (c b u) -> p c b u", c=H_PASSES, u=2),
             in_=hk_t[:].rearrange("p c u b -> p c b u"),
         )
-        spread_base(0)
-        spread_base(1)
-        col_t_ps = psum_tr.tile([I, B], BF16, name="col_t_ps", tag="transposed")
-        col_t = const.tile([I, B], BF16)
-        nc.tensor.transpose(col_t_ps[:], col_sb[:], ident_bf16[:])
-        for g in range(2, BASE_AHEAD):
-            keep_base(g - 2)
-            spread_base(g)
-
         hk_codes = const.tile([P, H_PASSES * B], U32, align_bytes=64)
         hk_scales = const.tile([P, H_PASSES * B], U8, align_bytes=64)
-        kw2_grouped = const.tile([P, H_PASSES, K, PACK], BF16, align_bytes=64)
+        kw2_grouped = const.tile([P, H_PASSES, PACK, P, PACK], BF16, align_bytes=64)
         kw2_codes = const.tile([P, H_PASSES, K], U32, align_bytes=64)
         kw2_scales = const.tile([P, H_PASSES, K], U8, align_bytes=64)
-        for c in range(H_PASSES):
-            interleave(nc.vector.tensor_copy, kw2_grouped[:, c], kw2_raw[:, c])
-        for c in range(H_PASSES):
+
+        def interleave_kw2(copy, c, t0, t1):
+            copy(
+                out=kw2_grouped[:, c, t0:t1],
+                in_=kw2_raw[:, c].rearrange("p j (m t) -> p t m j", t=PACK)[:, t0:t1],
+            )
+
+        def quantise_kw2(c):
             nc.vector.quantize_mx(
                 out=kw2_codes[:, c, :].bitcast(FP8X4),
                 scales=kw2_scales[:, c, :],
-                in_=kw2_grouped[:, c].rearrange("p n j -> p (n j)"),
+                in_=kw2_grouped[:, c].rearrange("p t m j -> p (t m j)"),
             )
-        nc.vector.quantize_mx(out=hk_codes[:].bitcast(FP8X4), scales=hk_scales[:], in_=hk_grouped[:])
 
-        nc.vector.tensor_copy(out=col_t[:], in_=col_t_ps[:])
-        nc.tensor.transpose(col_ps[:], col_t[:], ident_bf16[:])
-        nc.vector.tensor_copy(out=row_f32[:], in_=row_sb[:])
-
-        pre_acc = psum_acc.tile([B, K], F32, name="acc", tag="acc")
         for c in range(H_PASSES):
-            nc.tensor.matmul_mx(
-                out=pre_acc[:],
-                lhsT=hk_codes[:, c * B : (c + 1) * B].bitcast(FP8X4),
-                lhsT_scale=hk_scales[:, c * B : (c + 1) * B],
-                rhs=kw2_codes[:, c, :].bitcast(FP8X4),
-                rhs_scale=kw2_scales[:, c, :],
-                start=(c == 0),
-                stop=(c == H_PASSES - 1),
-            )
-        regroup(0, nc.scalar.copy)
-        keep_base(BASE_AHEAD - 2)
-        keep_base(BASE_AHEAD - 1)
-        regroup(1, nc.vector.tensor_copy)
+            interleave_kw2(nc.scalar.copy, c, 0, 1)
+            interleave_kw2(nc.vector.tensor_copy, c, 1, PACK)
+        nc.vector.quantize_mx(out=hk_codes[:].bitcast(FP8X4), scales=hk_scales[:], in_=hk_grouped[:])
+        for c in range(H_PASSES):
+            quantise_kw2(c)
 
-        pre = const.tile([B, K], F32)
-        coeff = const.tile([B, K], F32)
-        coeff_bf16 = const.tile([B, PACK, P], BF16)
-        nc.vector.tensor_tensor(out=pre[:], in0=pre_acc[:], in1=kb2_bc[:], op=ADD)
-        nc.scalar.activation(
-            out=coeff_bf16[:], in_=pre[:].rearrange("b (p t) -> b t p", t=PACK), func=TANH
-        )
-        quantise(0)
-        quantise(1)
-        coeff_t = psum_tr.tile([P, PACK, B], BF16, name="coeff_t", tag="transposed")
+        pre = psum_head.tile([P, PACK, B], F32, name="pre", tag="head")
         for t in range(PACK):
-            nc.tensor.transpose(coeff_t[:, t, :], coeff_bf16[:, t, :], ident_bf16[:])
+            for c in range(H_PASSES):
+                nc.tensor.matmul_mx(
+                    out=pre[:, t, :],
+                    lhsT=kw2_codes[:, c, t * P : (t + 1) * P].bitcast(FP8X4),
+                    lhsT_scale=kw2_scales[:, c, t * P : (t + 1) * P],
+                    rhs=hk_codes[:, c * B : (c + 1) * B].bitcast(FP8X4),
+                    rhs_scale=hk_scales[:, c * B : (c + 1) * B],
+                    start=(c == 0),
+                    stop=(c == H_PASSES - 1),
+                )
+        for u in range(AHEAD):
+            begin(u)
+        on_scalar(0)
+        on_vector(0)
+        coeff_t = const.tile([P, PACK, B], F32)
+        for t in range(PACK):
+            nc.scalar.activation(
+                out=coeff_t[:, t, :], in_=pre[:, t, :], func=TANH, bias=kb2_t[:, t : t + 1]
+            )
+
+        base_col_ps = psum_head.tile([P, 2, P], BF16, name="base_col_ps", tag="head")
+        nc.tensor.transpose(base_col_ps[:, 0, :], base_sb[:], ident_bf16[:])
+        nc.tensor.transpose(base_col_ps[:, 1, :], col_sb[:], ident_bf16[:])
         coeff_grouped = const.tile([P, B, PACK], BF16, align_bytes=64)
         nc.vector.tensor_copy(out=coeff_grouped[:], in_=coeff_t[:].rearrange("p t b -> p b t"))
+        quantise(0)
         nc.vector.quantize_mx(
             out=coeff_codes[:].bitcast(FP8X4),
             scales=coeff_scales[:],
             in_=coeff_grouped[:].rearrange("p b t -> p (b t)"),
         )
-        regroup_shared(2)
-        regroup_shared(3)
-
+        nc.vector.tensor_copy(out=base_col_t[:], in_=base_col_ps[:])
+        nc.vector.tensor_copy(out=row_f32[:], in_=row_sb[:])
+        on_scalar(1)
+        on_vector(1)
+        for u in range(FIRST, AHEAD):
+            on_gpsimd(u)
+            on_scalar(u)
+        quantise(1)
+        on_vector(2)
         multiply(0)
-        multiply(1)
-        spread_base(BASE_AHEAD)
-        spread_base(BASE_AHEAD + 1)
-        quantise(2)
-        multiply(2)
-        add_base(0)
+        for u in range(LOAD_UNITS, AHEAD, LOAD_UNITS):
+            load(u // LOAD_UNITS - 1 + RAW_BUFS, 1)
+
+        coeff_ps = psum_head.tile([B, PACK, P], F32, name="coeff_ps", tag="head")
+        coeff = const.tile([B, K], F32)
+
         for u in range(N_UNITS):
-            if u + REGROUP_AHEAD < N_UNITS:
-                regroup_shared(u + REGROUP_AHEAD)
-            if u + REGROUP_AHEAD == N_UNITS:
-                nc.scalar.activation(out=coeff[:], in_=pre[:], func=TANH)
-                nc.sync.dma_start(out=out_1, in_=coeff[:])
-            g = u // UNITS_PER_BANK + BASE_AHEAD
-            if u % UNITS_PER_BANK == 0 and g < N_BANKS:
-                keep_base(g)
-            if FIRST_UNITS <= u + QUANTISE_AHEAD < N_UNITS:
-                quantise(u + QUANTISE_AHEAD)
-                multiply(u + QUANTISE_AHEAD)
-            if u % UNITS_PER_BANK == 1 and g + 2 < N_BANKS:
-                spread_base(g + 2)
+            if u + AHEAD < N_UNITS:
+                begin(u + AHEAD)
+                on_gpsimd(u + AHEAD)
+                on_scalar(u + AHEAD)
+            l = (u + AHEAD) // LOAD_UNITS - 1 + RAW_BUFS
+            if (u + AHEAD) % LOAD_UNITS == 0 and RAW_BUFS <= l < N_LOADS:
+                load(l, 1)
+            add_base(u)
+            if u > 0:
+                turn(u - 1)
             if u + 1 < N_UNITS:
-                add_base(u + 1)
-            apply_gains(u)
+                multiply(u + 1)
+            if u == 1:
+                for t in range(PACK):
+                    nc.tensor.transpose(coeff_ps[:, t, :], coeff_t[:, t, :], ident_f32[:])
+                nc.scalar.copy(
+                    out=coeff[:].rearrange("b (p t) -> b p t", t=PACK),
+                    in_=coeff_ps[:].rearrange("b t p -> b p t"),
+                )
+                nc.sync.dma_start(out=out_1, in_=coeff[:])
+            if u + QUANTISE_AHEAD < N_UNITS:
+                quantise(u + QUANTISE_AHEAD)
+            if u + QUANTISE_AHEAD + 1 < N_UNITS:
+                on_vector(u + QUANTISE_AHEAD + 1)
+            if u > 0:
+                apply_row(u - 1)
+        turn(N_UNITS - 1)
+        apply_row(N_UNITS - 1)

@@ -31,7 +31,7 @@ RAW_BUFS = 10
 STORE_UNITS = 2
 RUN = 4
 GPSIMD_COLUMNS = 128
-VECTOR_COLUMNS = 128
+VECTOR_COLUMNS = 192
 AHEAD = 4
 QUANTISE_AHEAD = 2
 FIRST = 2

@@ -25,10 +25,10 @@ FLOPS = 2 * B * H * K + 2 * B * K * N
 UNIT = 512
 N_UNITS = N // UNIT
 ROWS = UNIT // I
-LOAD_UNITS = 2
+LOAD_UNITS = 4
 N_LOADS = N_UNITS // LOAD_UNITS
-RAW_BUFS = 10
-STORE_UNITS = 2
+RAW_BUFS = 5
+STORE_UNITS = 4
 RUN = 4
 GPSIMD_COLUMNS = 128
 VECTOR_COLUMNS = 192
@@ -60,7 +60,7 @@ def tile_structuredternaryfactorgenerator_pa_kernel(
         grouped_pool = ctx.enter_context(tc.tile_pool(name="grouped", bufs=8))
         mx_pool = ctx.enter_context(tc.tile_pool(name="mx", bufs=5))
         mid_pool = ctx.enter_context(tc.tile_pool(name="mid", bufs=3))
-        weight_pool = ctx.enter_context(tc.tile_pool(name="weight", bufs=4))
+        weight_pool = ctx.enter_context(tc.tile_pool(name="weight", bufs=3))
         psum_acc = ctx.enter_context(tc.psum_pool(name="acc", bufs=3))
         psum_turned = ctx.enter_context(tc.psum_pool(name="turned", bufs=3))
         psum_head = ctx.enter_context(tc.psum_pool(name="head", bufs=2))
@@ -281,8 +281,6 @@ def tile_structuredternaryfactorgenerator_pa_kernel(
         quantise(1)
         on_vector(2)
         multiply(0)
-        for u in range(LOAD_UNITS, AHEAD, LOAD_UNITS):
-            load(u // LOAD_UNITS - 1 + RAW_BUFS, 1)
 
         coeff_ps = psum_head.tile([B, PACK, P], F32, name="coeff_ps", tag="head")
         coeff = const.tile([B, K], F32)

@@ -27,12 +27,13 @@ N_UNITS = N // UNIT
 ROWS = UNIT // I
 LOAD_UNITS = 4
 N_LOADS = N_UNITS // LOAD_UNITS
+FIRST_PIECES = [[1, 1, 2], [2, 2], [2, 2], [4]]
 RAW_BUFS = 5
 STORE_UNITS = 4
 RUN = 4
 GPSIMD_COLUMNS = 128
-VECTOR_COLUMNS = 192
-AHEAD = 4
+VECTOR_COLUMNS = 144
+AHEAD = 3
 QUANTISE_AHEAD = 2
 FIRST = 2
 
@@ -57,7 +58,7 @@ def tile_structuredternaryfactorgenerator_pa_kernel(
         ctx.enter_context(tc.manual_schedule())
         const = ctx.enter_context(tc.tile_pool(name="const", bufs=1))
         raw_pool = ctx.enter_context(tc.tile_pool(name="raw", bufs=RAW_BUFS))
-        grouped_pool = ctx.enter_context(tc.tile_pool(name="grouped", bufs=8))
+        grouped_pool = ctx.enter_context(tc.tile_pool(name="grouped", bufs=5))
         mx_pool = ctx.enter_context(tc.tile_pool(name="mx", bufs=5))
         mid_pool = ctx.enter_context(tc.tile_pool(name="mid", bufs=3))
         weight_pool = ctx.enter_context(tc.tile_pool(name="weight", bufs=3))
@@ -75,12 +76,14 @@ def tile_structuredternaryfactorgenerator_pa_kernel(
 
         def load(l, pieces):
             raw[l] = raw_pool.tile([P, PACK, LOAD_UNITS * UNIT], BF16, name="raw", tag="raw")
-            width = LOAD_UNITS * UNIT // pieces
-            for offset in range(0, LOAD_UNITS * UNIT, width):
+            offset = 0
+            for units in pieces:
+                width = units * UNIT
                 start = l * LOAD_UNITS * UNIT + offset
                 nc.sync.dma_start(
                     out=raw[l][:, :, offset : offset + width], in_=bases_rows[:, :, start : start + width]
                 )
+                offset += width
 
         def unit_rows(u):
             offset = u % LOAD_UNITS * UNIT
@@ -191,16 +194,16 @@ def tile_structuredternaryfactorgenerator_pa_kernel(
         base_sb = const.tile([O, I], BF16)
         col_sb = const.tile([B, I], BF16)
         row_sb = const.tile([B, O], BF16)
+        nc.sync.dma_start(out=kw2_raw[:, 0], in_=kw2_rows[0])
         nc.sync.dma_start(out=hk_sb[:], in_=hk)
-        for c in range(H_PASSES):
-            nc.sync.dma_start(out=kw2_raw[:, c], in_=kw2_rows[c])
+        nc.sync.dma_start(out=kw2_raw[:, 1], in_=kw2_rows[1])
         nc.sync.dma_start(out=kb2_t[:], in_=kb2.rearrange("(p t) -> p t", t=PACK))
-        load(0, LOAD_UNITS)
         nc.sync.dma_start(out=base_sb[:], in_=base)
         nc.sync.dma_start(out=col_sb[:], in_=col)
         nc.sync.dma_start(out=row_sb[:], in_=row)
+        load(0, FIRST_PIECES[0])
         for l in range(1, RAW_BUFS):
-            load(l, 1)
+            load(l, FIRST_PIECES[min(l, len(FIRST_PIECES) - 1)])
 
         hk_words = hk_sb[:].bitcast(F32).rearrange("b (c p u) -> b c u p", c=H_PASSES, u=2)
         hk_t = psum_head.tile([P, H_PASSES, 2, B], F32, name="hk_t", tag="head")
@@ -208,10 +211,6 @@ def tile_structuredternaryfactorgenerator_pa_kernel(
             for u in range(2):
                 nc.tensor.transpose(hk_t[:, c, u, :], hk_words[:, c, u, :], ident_f32[:])
         hk_grouped = const.tile([P, H_PASSES * B * PACK], BF16, align_bytes=64)
-        nc.scalar.copy(
-            out=hk_grouped[:].bitcast(F32).rearrange("p (c b u) -> p c b u", c=H_PASSES, u=2),
-            in_=hk_t[:].rearrange("p c u b -> p c b u"),
-        )
         hk_codes = const.tile([P, H_PASSES * B], U32, align_bytes=64)
         hk_scales = const.tile([P, H_PASSES * B], U8, align_bytes=64)
         kw2_grouped = const.tile([P, H_PASSES, PACK, P, PACK], BF16, align_bytes=64)
@@ -231,18 +230,27 @@ def tile_structuredternaryfactorgenerator_pa_kernel(
                 in_=kw2_grouped[:, c].rearrange("p t m j -> p (t m j)"),
             )
 
+        pre = [
+            psum_acc.tile([I, ROWS, B], F32, name="pre", tag="acc")
+            if t < PACK - 1
+            else psum_turned.tile([B, ROWS, I], F32, name="pre_last", tag="turned")
+            for t in range(PACK)
+        ]
         for c in range(H_PASSES):
             interleave_kw2(nc.scalar.copy, c, 0, 1)
             interleave_kw2(nc.vector.tensor_copy, c, 1, PACK)
-        nc.vector.quantize_mx(out=hk_codes[:].bitcast(FP8X4), scales=hk_scales[:], in_=hk_grouped[:])
-        for c in range(H_PASSES):
             quantise_kw2(c)
-
-        pre = psum_head.tile([P, PACK, B], F32, name="pre", tag="head")
-        for t in range(PACK):
-            for c in range(H_PASSES):
+            if c == 0:
+                nc.scalar.copy(
+                    out=hk_grouped[:].bitcast(F32).rearrange("p (c b u) -> p c b u", c=H_PASSES, u=2),
+                    in_=hk_t[:].rearrange("p c u b -> p c b u"),
+                )
+                nc.vector.quantize_mx(
+                    out=hk_codes[:].bitcast(FP8X4), scales=hk_scales[:], in_=hk_grouped[:]
+                )
+            for t in range(PACK):
                 nc.tensor.matmul_mx(
-                    out=pre[:, t, :],
+                    out=pre[t][:, 0, :],
                     lhsT=kw2_codes[:, c, t * P : (t + 1) * P].bitcast(FP8X4),
                     lhsT_scale=kw2_scales[:, c, t * P : (t + 1) * P],
                     rhs=hk_codes[:, c * B : (c + 1) * B].bitcast(FP8X4),
@@ -254,10 +262,12 @@ def tile_structuredternaryfactorgenerator_pa_kernel(
             begin(u)
         on_scalar(0)
         on_vector(0)
+        quantise(0)
+        on_vector(1)
         coeff_t = const.tile([P, PACK, B], F32)
         for t in range(PACK):
             nc.scalar.activation(
-                out=coeff_t[:, t, :], in_=pre[:, t, :], func=TANH, bias=kb2_t[:, t : t + 1]
+                out=coeff_t[:, t, :], in_=pre[t][:, 0, :], func=TANH, bias=kb2_t[:, t : t + 1]
             )
 
         base_col_ps = psum_head.tile([P, 2, P], BF16, name="base_col_ps", tag="head")
@@ -265,16 +275,14 @@ def tile_structuredternaryfactorgenerator_pa_kernel(
         nc.tensor.transpose(base_col_ps[:, 1, :], col_sb[:], ident_bf16[:])
         coeff_grouped = const.tile([P, B, PACK], BF16, align_bytes=64)
         nc.vector.tensor_copy(out=coeff_grouped[:], in_=coeff_t[:].rearrange("p t b -> p b t"))
-        quantise(0)
+        nc.vector.tensor_copy(out=base_col_t[:], in_=base_col_ps[:])
         nc.vector.quantize_mx(
             out=coeff_codes[:].bitcast(FP8X4),
             scales=coeff_scales[:],
             in_=coeff_grouped[:].rearrange("p b t -> p (b t)"),
         )
-        nc.vector.tensor_copy(out=base_col_t[:], in_=base_col_ps[:])
-        nc.vector.tensor_copy(out=row_f32[:], in_=row_sb[:])
         on_scalar(1)
-        on_vector(1)
+        nc.scalar.copy(out=row_f32[:], in_=row_sb[:])
         for u in range(FIRST, AHEAD):
             on_gpsimd(u)
             on_scalar(u)
@@ -286,19 +294,20 @@ def tile_structuredternaryfactorgenerator_pa_kernel(
         coeff = const.tile([B, K], F32)
 
         for u in range(N_UNITS):
+            if u > 0:
+                apply_row(u - 1)
             if u + AHEAD < N_UNITS:
                 begin(u + AHEAD)
                 on_gpsimd(u + AHEAD)
                 on_scalar(u + AHEAD)
             l = (u + AHEAD) // LOAD_UNITS - 1 + RAW_BUFS
             if (u + AHEAD) % LOAD_UNITS == 0 and RAW_BUFS <= l < N_LOADS:
-                load(l, 1)
+                load(l, [LOAD_UNITS])
             add_base(u)
-            if u > 0:
-                turn(u - 1)
             if u + 1 < N_UNITS:
                 multiply(u + 1)
-            if u == 1:
+            turn(u)
+            if u == N_UNITS - AHEAD:
                 for t in range(PACK):
                     nc.tensor.transpose(coeff_ps[:, t, :], coeff_t[:, t, :], ident_f32[:])
                 nc.scalar.copy(
@@ -310,7 +319,4 @@ def tile_structuredternaryfactorgenerator_pa_kernel(
                 quantise(u + QUANTISE_AHEAD)
             if u + QUANTISE_AHEAD + 1 < N_UNITS:
                 on_vector(u + QUANTISE_AHEAD + 1)
-            if u > 0:
-                apply_row(u - 1)
-        turn(N_UNITS - 1)
         apply_row(N_UNITS - 1)

@@ -58,7 +58,7 @@ def tile_structuredternaryfactorgenerator_pa_kernel(
         ctx.enter_context(tc.manual_schedule())
         const = ctx.enter_context(tc.tile_pool(name="const", bufs=1))
         raw_pool = ctx.enter_context(tc.tile_pool(name="raw", bufs=RAW_BUFS))
-        grouped_pool = ctx.enter_context(tc.tile_pool(name="grouped", bufs=5))
+        grouped_pool = ctx.enter_context(tc.tile_pool(name="grouped", bufs=4))
         mx_pool = ctx.enter_context(tc.tile_pool(name="mx", bufs=5))
         mid_pool = ctx.enter_context(tc.tile_pool(name="mid", bufs=3))
         weight_pool = ctx.enter_context(tc.tile_pool(name="weight", bufs=3))
@@ -292,6 +292,18 @@ def tile_structuredternaryfactorgenerator_pa_kernel(
 
         coeff_ps = psum_head.tile([B, PACK, P], F32, name="coeff_ps", tag="head")
         coeff = const.tile([B, K], F32)
+        busy = psum_head.tile([B, UNIT], F32, name="busy", tag="head")
+
+        def keep_clock(u):
+            nc.tensor.matmul_mx(
+                out=busy[:],
+                lhsT=coeff_codes[:].bitcast(FP8X4),
+                lhsT_scale=coeff_scales[:],
+                rhs=codes[u][:].bitcast(FP8X4),
+                rhs_scale=scales[u][:],
+                start=True,
+                stop=True,
+            )
 
         for u in range(N_UNITS):
             if u > 0:
@@ -306,6 +318,7 @@ def tile_structuredternaryfactorgenerator_pa_kernel(
             add_base(u)
             if u + 1 < N_UNITS:
                 multiply(u + 1)
+                keep_clock(u + 1)
             turn(u)
             if u == N_UNITS - AHEAD:
                 for t in range(PACK):

@@ -32,10 +32,11 @@ RAW_BUFS = 5
 STORE_UNITS = 4
 RUN = 4
 GPSIMD_COLUMNS = 128
-VECTOR_COLUMNS = 144
+VECTOR_COLUMNS = 152
 AHEAD = 3
 QUANTISE_AHEAD = 2
-FIRST = 2
+FIRST_VECTOR_COLUMNS = 288
+FIRST = 3
 
 
 def interleave(copy, grouped, rows):
@@ -61,7 +62,7 @@ def tile_structuredternaryfactorgenerator_pa_kernel(
         grouped_pool = ctx.enter_context(tc.tile_pool(name="grouped", bufs=4))
         mx_pool = ctx.enter_context(tc.tile_pool(name="mx", bufs=5))
         mid_pool = ctx.enter_context(tc.tile_pool(name="mid", bufs=3))
-        weight_pool = ctx.enter_context(tc.tile_pool(name="weight", bufs=3))
+        weight_pool = ctx.enter_context(tc.tile_pool(name="weight", bufs=5))
         psum_acc = ctx.enter_context(tc.psum_pool(name="acc", bufs=3))
         psum_turned = ctx.enter_context(tc.psum_pool(name="turned", bufs=3))
         psum_head = ctx.enter_context(tc.psum_pool(name="head", bufs=2))
@@ -95,6 +96,8 @@ def tile_structuredternaryfactorgenerator_pa_kernel(
             )
 
         def on_gpsimd(u):
+            if u < FIRST:
+                return
             nc.gpsimd.tensor_scalar(
                 out=grouped[u][:, :GPSIMD_COLUMNS, :],
                 in0=unit_rows(u)[:, :, :GPSIMD_COLUMNS].rearrange("p j w -> p w j"),
@@ -109,13 +112,13 @@ def tile_structuredternaryfactorgenerator_pa_kernel(
 
         def on_vector(u):
             if u < FIRST:
-                on_engine(nc.vector.tensor_copy, u, 0, UNIT // 2)
+                on_engine(nc.vector.tensor_copy, u, 0, FIRST_VECTOR_COLUMNS)
             else:
                 on_engine(nc.vector.tensor_copy, u, GPSIMD_COLUMNS, GPSIMD_COLUMNS + VECTOR_COLUMNS)
 
         def on_scalar(u):
             if u < FIRST:
-                on_engine(nc.scalar.copy, u, UNIT // 2, UNIT)
+                on_engine(nc.scalar.copy, u, FIRST_VECTOR_COLUMNS, UNIT)
             else:
                 on_engine(nc.scalar.copy, u, GPSIMD_COLUMNS + VECTOR_COLUMNS, UNIT)
 
@@ -240,6 +243,11 @@ def tile_structuredternaryfactorgenerator_pa_kernel(
             interleave_kw2(nc.scalar.copy, c, 0, 1)
             interleave_kw2(nc.vector.tensor_copy, c, 1, PACK)
             quantise_kw2(c)
+            if c == 1:
+                base_col_ps = psum_head.tile([P, 2, P], BF16, name="base_col_ps", tag="head")
+                nc.tensor.transpose(base_col_ps[:, 0, :], base_sb[:], ident_bf16[:])
+                nc.tensor.transpose(base_col_ps[:, 1, :], col_sb[:], ident_bf16[:])
+                nc.scalar.copy(out=base_col_t[:], in_=base_col_ps[:])
             if c == 0:
                 nc.scalar.copy(
                     out=hk_grouped[:].bitcast(F32).rearrange("p (c b u) -> p c b u", c=H_PASSES, u=2),
@@ -270,12 +278,8 @@ def tile_structuredternaryfactorgenerator_pa_kernel(
                 out=coeff_t[:, t, :], in_=pre[t][:, 0, :], func=TANH, bias=kb2_t[:, t : t + 1]
             )
 
-        base_col_ps = psum_head.tile([P, 2, P], BF16, name="base_col_ps", tag="head")
-        nc.tensor.transpose(base_col_ps[:, 0, :], base_sb[:], ident_bf16[:])
-        nc.tensor.transpose(base_col_ps[:, 1, :], col_sb[:], ident_bf16[:])
         coeff_grouped = const.tile([P, B, PACK], BF16, align_bytes=64)
         nc.vector.tensor_copy(out=coeff_grouped[:], in_=coeff_t[:].rearrange("p t b -> p b t"))
-        nc.vector.tensor_copy(out=base_col_t[:], in_=base_col_ps[:])
         nc.vector.quantize_mx(
             out=coeff_codes[:].bitcast(FP8X4),
             scales=coeff_scales[:],
@@ -283,7 +287,7 @@ def tile_structuredternaryfactorgenerator_pa_kernel(
         )
         on_scalar(1)
         nc.scalar.copy(out=row_f32[:], in_=row_sb[:])
-        for u in range(FIRST, AHEAD):
+        for u in range(2, AHEAD):
             on_gpsimd(u)
             on_scalar(u)
         quantise(1)

@@ -31,8 +31,8 @@ FIRST_PIECES = [[1, 1, 2], [2, 2], [2, 2], [4]]
 RAW_BUFS = 5
 STORE_UNITS = 4
 RUN = 4
-GPSIMD_COLUMNS = 128
-VECTOR_COLUMNS = 152
+GPSIMD_COLUMNS = 96
+VECTOR_COLUMNS = 176
 AHEAD = 3
 QUANTISE_AHEAD = 2
 FIRST_VECTOR_COLUMNS = 288

@@ -30,7 +30,8 @@ N_LOADS = N_UNITS // LOAD_UNITS
 FIRST_PIECES = [[1, 1, 2], [2, 2], [2, 2], [4]]
 RAW_BUFS = 5
 STORE_UNITS = 4
-RUN = 4
+VECTOR_RUN = 4
+SCALAR_RUN = 8
 GPSIMD_COLUMNS = 96
 VECTOR_COLUMNS = 176
 AHEAD = 3
@@ -39,10 +40,10 @@ FIRST_VECTOR_COLUMNS = 288
 FIRST = 3
 
 
-def interleave(copy, grouped, rows):
+def interleave(copy, grouped, rows, run):
     copy(
-        out=grouped.rearrange("p (c i) j -> p c j i", i=RUN),
-        in_=rows.rearrange("p j (c i) -> p c j i", i=RUN),
+        out=grouped.rearrange("p (c i) j -> p c j i", i=run),
+        in_=rows.rearrange("p j (c i) -> p c j i", i=run),
     )
 
 
@@ -107,20 +108,20 @@ def tile_structuredternaryfactorgenerator_pa_kernel(
                 op1=ADD,
             )
 
-        def on_engine(copy, u, start, stop):
-            interleave(copy, grouped[u][:, start:stop, :], unit_rows(u)[:, :, start:stop])
+        def on_engine(copy, u, start, stop, run):
+            interleave(copy, grouped[u][:, start:stop, :], unit_rows(u)[:, :, start:stop], run)
 
         def on_vector(u):
             if u < FIRST:
-                on_engine(nc.vector.tensor_copy, u, 0, FIRST_VECTOR_COLUMNS)
+                on_engine(nc.vector.tensor_copy, u, 0, FIRST_VECTOR_COLUMNS, VECTOR_RUN)
             else:
-                on_engine(nc.vector.tensor_copy, u, GPSIMD_COLUMNS, GPSIMD_COLUMNS + VECTOR_COLUMNS)
+                on_engine(nc.vector.tensor_copy, u, GPSIMD_COLUMNS, GPSIMD_COLUMNS + VECTOR_COLUMNS, VECTOR_RUN)
 
         def on_scalar(u):
             if u < FIRST:
-                on_engine(nc.scalar.copy, u, FIRST_VECTOR_COLUMNS, UNIT)
+                on_engine(nc.scalar.copy, u, FIRST_VECTOR_COLUMNS, UNIT, SCALAR_RUN)
             else:
-                on_engine(nc.scalar.copy, u, GPSIMD_COLUMNS + VECTOR_COLUMNS, UNIT)
+                on_engine(nc.scalar.copy, u, GPSIMD_COLUMNS + VECTOR_COLUMNS, UNIT, SCALAR_RUN)
 
         def quantise(u):
             codes[u] = mx_pool.tile([P, UNIT], U32, name="codes", tag="codes", align_bytes=64)

from contextlib import ExitStack

import concourse.mybir as mybir
from concourse.masks import make_identity

F32 = mybir.dt.float32
BF16 = mybir.dt.bfloat16
U32 = mybir.dt.uint32
U8 = mybir.dt.uint8
FP8X4 = mybir.dt.float8_e4m3fn_x4
ADD = mybir.AluOpType.add
MULT = mybir.AluOpType.mult
TANH = mybir.ActivationFunctionType.Tanh
COPY = mybir.ActivationFunctionType.Copy

P = 128
PACK = 4
K_PASS = P * PACK

B, H, O, I, K = 128, 1024, 128, 128, 512
N = O * I
H_PASSES = H // K_PASS
FLOPS = 2 * B * H * K + 2 * B * K * N

UNIT = 512
N_UNITS = N // UNIT
ROWS = UNIT // I
LOAD_UNITS = 4
N_LOADS = N_UNITS // LOAD_UNITS
FIRST_PIECES = [[1, 1, 2], [2, 2], [2, 2], [4]]
RAW_BUFS = 5
STORE_UNITS = 4
VECTOR_RUN = 4
SCALAR_RUN = 8
GPSIMD_COLUMNS = 96
VECTOR_COLUMNS = 176
AHEAD = 3
QUANTISE_AHEAD = 2
FIRST_VECTOR_COLUMNS = 288
FIRST = 3


def interleave(copy, grouped, rows, run):
    copy(
        out=grouped.rearrange("p (c i) j -> p c j i", i=run),
        in_=rows.rearrange("p j (c i) -> p c j i", i=run),
    )


def tile_structuredternaryfactorgenerator_pa_kernel(
    tc, hk, kw2, kb2, bases, base, row, col, out_0, out_1
):
    nc = tc.nc

    bases_rows = bases.rearrange("(p j) o i -> p j (o i)", j=PACK)
    kw2_rows = kw2.rearrange("(c p j) n -> c p j n", c=H_PASSES, j=PACK)
    weight_out = out_0.rearrange("b o i -> b (o i)")

    with ExitStack() as ctx:
        ctx.enter_context(tc.manual_schedule())
        const = ctx.enter_context(tc.tile_pool(name="const", bufs=1))
        raw_pool = ctx.enter_context(tc.tile_pool(name="raw", bufs=RAW_BUFS))
        grouped_pool = ctx.enter_context(tc.tile_pool(name="grouped", bufs=4))
        mx_pool = ctx.enter_context(tc.tile_pool(name="mx", bufs=5))
        mid_pool = ctx.enter_context(tc.tile_pool(name="mid", bufs=3))
        weight_pool = ctx.enter_context(tc.tile_pool(name="weight", bufs=5))
        psum_acc = ctx.enter_context(tc.psum_pool(name="acc", bufs=3))
        psum_turned = ctx.enter_context(tc.psum_pool(name="turned", bufs=3))
        psum_head = ctx.enter_context(tc.psum_pool(name="head", bufs=2))

        raw, grouped, codes, scales, acc, mid, turned, weight = {}, {}, {}, {}, {}, {}, {}, {}
        ident_f32 = const.tile([P, P], F32)
        ident_bf16 = const.tile([P, P], BF16)
        coeff_codes = const.tile([P, B], U32, align_bytes=64)
        coeff_scales = const.tile([P, B], U8, align_bytes=64)
        row_f32 = const.tile([B, O], F32)
        base_col_t = const.tile([P, 2, P], F32)

        def load(l, pieces):
            raw[l] = raw_pool.tile([P, PACK, LOAD_UNITS * UNIT], BF16, name="raw", tag="raw")
            offset = 0
            for units in pieces:
                width = units * UNIT
                start = l * LOAD_UNITS * UNIT + offset
                nc.sync.dma_start(
                    out=raw[l][:, :, offset : offset + width], in_=bases_rows[:, :, start : start + width]
                )
                offset += width

        def unit_rows(u):
            offset = u % LOAD_UNITS * UNIT
            return raw[u // LOAD_UNITS][:, :, offset : offset + UNIT]

        def begin(u):
            grouped[u] = grouped_pool.tile(
                [P, UNIT, PACK], BF16, name="grouped", tag="grouped", align_bytes=64
            )

        def on_gpsimd(u):
            if u < FIRST:
                return
            nc.gpsimd.tensor_scalar(
                out=grouped[u][:, :GPSIMD_COLUMNS, :],
                in0=unit_rows(u)[:, :, :GPSIMD_COLUMNS].rearrange("p j w -> p w j"),
                scalar1=1.0,
                scalar2=0.0,
                op0=MULT,
                op1=ADD,
            )

        def on_engine(copy, u, start, stop, run):
            interleave(copy, grouped[u][:, start:stop, :], unit_rows(u)[:, :, start:stop], run)

        def on_vector(u):
            if u < FIRST:
                on_engine(nc.vector.tensor_copy, u, 0, FIRST_VECTOR_COLUMNS, VECTOR_RUN)
            else:
                on_engine(nc.vector.tensor_copy, u, GPSIMD_COLUMNS, GPSIMD_COLUMNS + VECTOR_COLUMNS, VECTOR_RUN)

        def on_scalar(u):
            if u < FIRST:
                on_engine(nc.scalar.copy, u, FIRST_VECTOR_COLUMNS, UNIT, SCALAR_RUN)
            else:
                on_engine(nc.scalar.copy, u, GPSIMD_COLUMNS + VECTOR_COLUMNS, UNIT, SCALAR_RUN)

        def quantise(u):
            codes[u] = mx_pool.tile([P, UNIT], U32, name="codes", tag="codes", align_bytes=64)
            scales[u] = mx_pool.tile([P, UNIT], U8, name="scales", tag="scales", align_bytes=64)
            nc.vector.quantize_mx(
                out=codes[u][:].bitcast(FP8X4),
                scales=scales[u][:],
                in_=grouped[u][:].rearrange("p w j -> p (w j)"),
            )

        def multiply(u):
            acc[u] = psum_acc.tile([I, ROWS, B], F32, name="acc", tag="acc")
            for r in range(ROWS):
                cols = slice(r * I, (r + 1) * I)
                nc.tensor.matmul_mx(
                    out=acc[u][:, r, :],
                    lhsT=codes[u][:, cols].bitcast(FP8X4),
                    lhsT_scale=scales[u][:, cols],
                    rhs=coeff_codes[:].bitcast(FP8X4),
                    rhs_scale=coeff_scales[:],
                    start=True,
                    stop=True,
                )

        def add_base(u):
            mid[u] = mid_pool.tile([I, ROWS, B], F32, name="mid", tag="mid")
            for r in range(ROWS):
                o = u * ROWS + r
                nc.vector.scalar_tensor_tensor(
                    out=mid[u][:, r, :],
                    in0=acc[u][:, r, :],
                    scalar=base_col_t[:, 0, o : o + 1],
                    in1=base_col_t[:, 1, :],
                    op0=ADD,
                    op1=MULT,
                )

        def turn(u):
            turned[u] = psum_turned.tile([B, ROWS, I], F32, name="turned", tag="turned")
            for r in range(ROWS):
                nc.tensor.transpose(turned[u][:, r, :], mid[u][:, r, :], ident_f32[:])

        def apply_row(u):
            s, offset = u // STORE_UNITS, u % STORE_UNITS * UNIT
            if offset == 0:
                weight[s] = weight_pool.tile([B, STORE_UNITS * UNIT], F32, name="weight", tag="weight")
            for r in range(ROWS):
                o = u * ROWS + r
                nc.scalar.activation(
                    out=weight[s][:, offset + r * I : offset + (r + 1) * I],
                    in_=turned[u][:, r, :],
                    func=COPY,
                    scale=row_f32[:, o : o + 1],
                )
            if u >= N_UNITS - STORE_UNITS:
                nc.sync.dma_start(
                    out=weight_out[:, u * UNIT : (u + 1) * UNIT], in_=weight[s][:, offset : offset + UNIT]
                )
            elif offset == (STORE_UNITS - 1) * UNIT:
                nc.sync.dma_start(
                    out=weight_out[:, (u + 1 - STORE_UNITS) * UNIT : (u + 1) * UNIT], in_=weight[s][:]
                )

        warm = const.tile([P, 1], F32)
        warmed = const.tile([P, 1], F32)
        nc.vector.memset(warm[:], 0.0)
        nc.scalar.activation(out=warmed[:], in_=warm[:], func=TANH)
        make_identity(nc, ident_f32[:])
        make_identity(nc, ident_bf16[:])

        hk_sb = const.tile([B, H], BF16)
        kw2_raw = const.tile([P, H_PASSES, PACK, K], BF16)
        kb2_t = const.tile([P, PACK], BF16)
        base_sb = const.tile([O, I], BF16)
        col_sb = const.tile([B, I], BF16)
        row_sb = const.tile([B, O], BF16)
        nc.sync.dma_start(out=kw2_raw[:, 0], in_=kw2_rows[0])
        nc.sync.dma_start(out=hk_sb[:], in_=hk)
        nc.sync.dma_start(out=kw2_raw[:, 1], in_=kw2_rows[1])
        nc.sync.dma_start(out=kb2_t[:], in_=kb2.rearrange("(p t) -> p t", t=PACK))
        nc.sync.dma_start(out=base_sb[:], in_=base)
        nc.sync.dma_start(out=col_sb[:], in_=col)
        nc.sync.dma_start(out=row_sb[:], in_=row)
        load(0, FIRST_PIECES[0])
        for l in range(1, RAW_BUFS):
            load(l, FIRST_PIECES[min(l, len(FIRST_PIECES) - 1)])

        hk_words = hk_sb[:].bitcast(F32).rearrange("b (c p u) -> b c u p", c=H_PASSES, u=2)
        hk_t = psum_head.tile([P, H_PASSES, 2, B], F32, name="hk_t", tag="head")
        for c in range(H_PASSES):
            for u in range(2):
                nc.tensor.transpose(hk_t[:, c, u, :], hk_words[:, c, u, :], ident_f32[:])
        hk_grouped = const.tile([P, H_PASSES * B * PACK], BF16, align_bytes=64)
        hk_codes = const.tile([P, H_PASSES * B], U32, align_bytes=64)
        hk_scales = const.tile([P, H_PASSES * B], U8, align_bytes=64)
        kw2_grouped = const.tile([P, H_PASSES, PACK, P, PACK], BF16, align_bytes=64)
        kw2_codes = const.tile([P, H_PASSES, K], U32, align_bytes=64)
        kw2_scales = const.tile([P, H_PASSES, K], U8, align_bytes=64)

        def interleave_kw2(copy, c, t0, t1):
            copy(
                out=kw2_grouped[:, c, t0:t1],
                in_=kw2_raw[:, c].rearrange("p j (m t) -> p t m j", t=PACK)[:, t0:t1],
            )

        def quantise_kw2(c):
            nc.vector.quantize_mx(
                out=kw2_codes[:, c, :].bitcast(FP8X4),
                scales=kw2_scales[:, c, :],
                in_=kw2_grouped[:, c].rearrange("p t m j -> p (t m j)"),
            )

        pre = [
            psum_acc.tile([I, ROWS, B], F32, name="pre", tag="acc")
            if t < PACK - 1
            else psum_turned.tile([B, ROWS, I], F32, name="pre_last", tag="turned")
            for t in range(PACK)
        ]
        for c in range(H_PASSES):
            interleave_kw2(nc.scalar.copy, c, 0, 1)
            interleave_kw2(nc.vector.tensor_copy, c, 1, PACK)
            quantise_kw2(c)
            if c == 1:
                base_col_ps = psum_head.tile([P, 2, P], BF16, name="base_col_ps", tag="head")
                nc.tensor.transpose(base_col_ps[:, 0, :], base_sb[:], ident_bf16[:])
                nc.tensor.transpose(base_col_ps[:, 1, :], col_sb[:], ident_bf16[:])
                nc.scalar.copy(out=base_col_t[:], in_=base_col_ps[:])
            if c == 0:
                nc.scalar.copy(
                    out=hk_grouped[:].bitcast(F32).rearrange("p (c b u) -> p c b u", c=H_PASSES, u=2),
                    in_=hk_t[:].rearrange("p c u b -> p c b u"),
                )
                nc.vector.quantize_mx(
                    out=hk_codes[:].bitcast(FP8X4), scales=hk_scales[:], in_=hk_grouped[:]
                )
            for t in range(PACK):
                nc.tensor.matmul_mx(
                    out=pre[t][:, 0, :],
                    lhsT=kw2_codes[:, c, t * P : (t + 1) * P].bitcast(FP8X4),
                    lhsT_scale=kw2_scales[:, c, t * P : (t + 1) * P],
                    rhs=hk_codes[:, c * B : (c + 1) * B].bitcast(FP8X4),
                    rhs_scale=hk_scales[:, c * B : (c + 1) * B],
                    start=(c == 0),
                    stop=(c == H_PASSES - 1),
                )
        for u in range(AHEAD):
            begin(u)
        on_scalar(0)
        on_vector(0)
        quantise(0)
        on_vector(1)
        coeff_t = const.tile([P, PACK, B], F32)
        for t in range(PACK):
            nc.scalar.activation(
                out=coeff_t[:, t, :], in_=pre[t][:, 0, :], func=TANH, bias=kb2_t[:, t : t + 1]
            )

        coeff_grouped = const.tile([P, B, PACK], BF16, align_bytes=64)
        nc.vector.tensor_copy(out=coeff_grouped[:], in_=coeff_t[:].rearrange("p t b -> p b t"))
        nc.vector.quantize_mx(
            out=coeff_codes[:].bitcast(FP8X4),
            scales=coeff_scales[:],
            in_=coeff_grouped[:].rearrange("p b t -> p (b t)"),
        )
        on_scalar(1)
        nc.scalar.copy(out=row_f32[:], in_=row_sb[:])
        for u in range(2, AHEAD):
            on_gpsimd(u)
            on_scalar(u)
        quantise(1)
        on_vector(2)
        multiply(0)

        coeff_ps = psum_head.tile([B, PACK, P], F32, name="coeff_ps", tag="head")
        coeff = const.tile([B, K], F32)
        busy = psum_head.tile([B, UNIT], F32, name="busy", tag="head")

        def keep_clock(u):
            nc.tensor.matmul_mx(
                out=busy[:],
                lhsT=coeff_codes[:].bitcast(FP8X4),
                lhsT_scale=coeff_scales[:],
                rhs=codes[u][:].bitcast(FP8X4),
                rhs_scale=scales[u][:],
                start=True,
                stop=True,
            )

        for u in range(N_UNITS):
            if u > 0:
                apply_row(u - 1)
            if u + AHEAD < N_UNITS:
                begin(u + AHEAD)
                on_gpsimd(u + AHEAD)
                on_scalar(u + AHEAD)
            l = (u + AHEAD) // LOAD_UNITS - 1 + RAW_BUFS
            if (u + AHEAD) % LOAD_UNITS == 0 and RAW_BUFS <= l < N_LOADS:
                load(l, [LOAD_UNITS])
            add_base(u)
            if u + 1 < N_UNITS:
                multiply(u + 1)
                keep_clock(u + 1)
            turn(u)
            if u == N_UNITS - AHEAD:
                for t in range(PACK):
                    nc.tensor.transpose(coeff_ps[:, t, :], coeff_t[:, t, :], ident_f32[:])
                nc.scalar.copy(
                    out=coeff[:].rearrange("b (p t) -> b p t", t=PACK),
                    in_=coeff_ps[:].rearrange("b t p -> b p t"),
                )
                nc.sync.dma_start(out=out_1, in_=coeff[:])
            if u + QUANTISE_AHEAD < N_UNITS:
                quantise(u + QUANTISE_AHEAD)
            if u + QUANTISE_AHEAD + 1 < N_UNITS:
                on_vector(u + QUANTISE_AHEAD + 1)
        apply_row(N_UNITS - 1)
